import numpy as np
import ml_dtypes


def mxq(x, axis, fmt="e4m3"):
    dtype, down = {"e4m3": (ml_dtypes.float8_e4m3fn, 7), "e5m2": (ml_dtypes.float8_e5m2, 14)}[fmt]
    v = np.moveaxis(np.asarray(x, np.float32).astype(ml_dtypes.bfloat16).astype(np.float64), axis, -1)
    blocks = v.reshape(v.shape[:-1] + (-1, 32))
    amax = np.abs(blocks).max(-1, keepdims=True)
    byte = np.maximum(np.where(amax > 0, np.frexp(amax)[1] - 1 + 127, 0) - down, 1)
    scale = np.exp2(byte - 127.0)
    codes = (blocks / scale).astype(np.float32).astype(dtype).astype(np.float64)
    return np.moveaxis((codes * scale).reshape(v.shape), -1, axis)


WIDE = False


def mx_kscale(k):
    if not WIDE:
        return np.ones(k)
    levels = np.array([10, -10, 5, -5, 0])
    a = np.random.permutation(np.resize(levels, k // 512 * 4)).reshape(k // 512, 4)
    idx = np.arange(k)
    return np.exp2(a[idx // 512, idx % 128 // 32])


BF16 = ml_dtypes.bfloat16


def bf(x):
    return np.asarray(x, np.float32).astype(BF16)


def f64(x):
    return np.asarray(x).astype(np.float64)


E2M1 = np.array([0.0, 0.5, 1.0, 1.5, 2.0, 3.0, 4.0, 6.0, -0.0, -0.5, -1.0, -1.5, -2.0, -3.0, -4.0, -6.0])


def pack_weight(w, fmt):
    k, n = w.shape
    w = f64(bf(w)).reshape(k // 32, 32, n)
    amax = np.abs(w).max(1)
    if fmt == "e4m3":
        byte = np.frexp(amax)[1] - 1 + 127 - 7
    else:
        mant, ex = np.frexp(amax / 6.0)
        byte = np.where(mant > 0.5, ex, ex - 1) + 127
    byte = np.clip(np.where(amax > 0, byte, 1), 1, 254)
    scaled = (w * np.exp2(127.0 - byte)[:, None, :]).reshape(k, n).astype(np.float32)
    by_word = np.ascontiguousarray(scaled.reshape(k // 512, 128, 4, n).transpose(0, 1, 3, 2))
    if fmt == "e4m3":
        words = by_word.astype(ml_dtypes.float8_e4m3fn).view(np.uint8)
    else:
        c = by_word.astype(ml_dtypes.float4_e2m1fn).view(np.uint8) & 0xF
        words = c[..., 0::2] | (c[..., 1::2] << 4)
    return np.ascontiguousarray(words), np.ascontiguousarray(byte.astype(np.uint8).reshape(k // 512, 16, n))


def unpack_weight(words, scales, fmt):
    g, p, n, _ = words.shape
    if fmt == "e4m3":
        vals = np.ascontiguousarray(words).view(ml_dtypes.float8_e4m3fn).astype(np.float64)
    else:
        nib = np.empty((g, p, n, 4), np.uint8)
        nib[..., 0::2] = words & 0xF
        nib[..., 1::2] = words >> 4
        vals = E2M1[nib]
    vals = vals * np.repeat(np.exp2(scales.astype(np.float64) - 127.0), 8, axis=1)[..., None]
    return vals.transpose(0, 1, 3, 2).reshape(g * 512, n)


B, N, D, P, C = 2, 512, 1024, 32, 5
G = 11 + C
O = P * G
OFFSET_MAX = 0.2
SCALE_MAX = 0.02
FMT = "e4m3"


def sigmoid(v):
    return 1.0 / (1.0 + np.exp(-v))


def silu(v):
    return v / (1.0 + np.exp(-v))


def setup_inputs():
    s = mx_kscale(D)
    xyzs = bf(np.random.standard_normal((B, N, 3)) * 0.25)
    latents = bf(np.random.standard_normal((B, N, D)) * s)
    W1_words, W1_scales = pack_weight(np.random.standard_normal((D, O)) / np.sqrt(D) / s[:, None], FMT)
    b1 = bf(np.random.standard_normal(O) * 0.3)
    W2_words, W2_scales = pack_weight(np.random.standard_normal((O, O)) * 2.5 / np.sqrt(O), FMT)
    b2 = bf(np.random.standard_normal(O) * 0.5)
    return {"xyzs": xyzs,
            "latents": latents,
            "W1_words": W1_words,
            "W1_scales": W1_scales,
            "b1": b1,
            "W2_words": W2_words,
            "W2_scales": W2_scales,
            "b2": b2}


def reference(xyzs, latents, W1_words, W1_scales, b1, W2_words, W2_scales, b2):
    xyzs = f64(xyzs)
    h = silu((mxq(f64(latents), 2, "e4m3") @ unpack_weight(W1_words, W1_scales, FMT)) + f64(b1))
    f = (mxq(h, 2, "e4m3") @ unpack_weight(W2_words, W2_scales, FMT)) + f64(b2)
    f = f.reshape(B, N, P, G)
    mean3D = xyzs[:, :, None, :] + sigmoid(f[..., 0:3]) * OFFSET_MAX
    opacity = sigmoid(f[..., 3:4])
    scales = sigmoid(f[..., 4:7]) * SCALE_MAX
    rot = f[..., 7:11]
    rot = rot / np.maximum(np.sqrt(np.sum(rot * rot, axis=-1, keepdims=True)), 1e-12)
    rgb = np.clip(f[..., 11:], -0.5, 0.5) + 0.5
    gaussians = np.concatenate([mean3D, opacity, scales, rot, rgb], axis=-1)
    return gaussians.reshape(B, N * P, G)

@@ -1,0 +1,240 @@
+from contextlib import ExitStack
+
+import concourse.mybir as mybir
+from concourse.masks import make_identity
+
+F32 = mybir.dt.float32
+BF16 = mybir.dt.bfloat16
+I32 = mybir.dt.int32
+U32 = mybir.dt.uint32
+U8 = mybir.dt.uint8
+FP8X4 = mybir.dt.float8_e4m3fn_x4
+ACT = mybir.ActivationFunctionType
+ALU = mybir.AluOpType
+AXIS = mybir.AxisListType
+
+P = 128
+PACK = 4
+K_PASS = P * PACK
+TOKENS = 2 * 512
+TILES = TOKENS // P
+D_IN = 1024
+WIDTH = 512
+PASSES_1 = D_IN // K_PASS
+GAUSSIANS = 32
+CHANNELS = 16
+OFFSET_MAX = 0.2
+SCALE_MAX = 0.02
+NORM_FLOOR = 1e-12
+QUADRANT = 32
+
+FLOPS = 2 * TOKENS * (D_IN * WIDTH + WIDTH * WIDTH)
+
+
+def tile_gaussianrenderer_kernel(
+    tc, xyzs, latents, W1_words, W1_scales, b1, W2_words, W2_scales, b2, out
+):
+    nc = tc.nc
+    lat_view = latents.flatten_outer_dims().rearrange("(p j) d -> p j d", j=TILES)
+    xyz_view = xyzs.flatten_outer_dims().rearrange("(p j) c -> p j c", j=TILES)
+    out_view = out.flatten_outer_dims().rearrange("(p j q) c -> p j (q c)", j=TILES, q=GAUSSIANS)
+
+    with ExitStack() as stack:
+        keep = stack.enter_context(tc.tile_pool(name="keep", bufs=1))
+        stage = stack.enter_context(tc.tile_pool(name="stage", bufs=3))
+        psum = stack.enter_context(tc.psum_pool(name="psum", bufs=2))
+
+        x_sb = keep.tile([P, TILES, D_IN], BF16)
+        x_codes = keep.tile([P, TILES, PASSES_1 * P], U32, align_bytes=64)
+        x_planes = keep.tile([P, TILES, PASSES_1 * P], U8, align_bytes=64)
+        h_codes = keep.tile([P, TILES, P], U32, align_bytes=64)
+        h_planes = keep.tile([P, TILES, P], U8, align_bytes=64)
+        w1_codes = keep.tile([P, PASSES_1, WIDTH], U32, align_bytes=64)
+        w1_planes = keep.tile([P, PASSES_1, WIDTH], U8, align_bytes=64)
+        w2_codes = keep.tile([P, WIDTH], U32, align_bytes=64)
+        w2_plane = keep.tile([P, WIDTH], U8, align_bytes=64)
+        bias_rows = keep.tile([P, 2, WIDTH], BF16)
+        ones = keep.tile([P, P], BF16)
+        b1_spread = keep.tile([P, PACK, P], F32)
+        b2_spread = keep.tile([P, WIDTH], F32)
+        xyz_sb = keep.tile([P, TILES, 3], BF16)
+        mean_base = keep.tile([P, TILES, 3], F32)
+        ident_f32 = keep.tile([P, P], F32)
+        ident_bf16 = keep.tile([P, P], BF16)
+        table_seed = keep.tile([P, 1], F32)
+        o_sb = keep.tile([P, TILES, WIDTH], F32)
+        norm_sq = keep.tile([P, TILES, GAUSSIANS], F32)
+        norm_inv = keep.tile([P, TILES, GAUSSIANS], F32)
+
+        nc.vector.memset(w1_planes[:].bitcast(I32), 0)
+        nc.vector.memset(w2_plane[:].bitcast(I32), 0)
+        nc.vector.memset(bias_rows[:], 0.0)
+        nc.vector.memset(ones[:], 1.0)
+        nc.vector.memset(table_seed[:], 0.0)
+        make_identity(nc, ident_f32[:])
+        make_identity(nc, ident_bf16[:])
+        nc.scalar.activation(out=table_seed[:], in_=table_seed[:], func=ACT.Silu)
+
+        nc.scalar.dma_start(out=bias_rows[0:1, 0, :], in_=b1.unsqueeze(0))
+        nc.scalar.dma_start(out=bias_rows[0:1, 1, :], in_=b2.unsqueeze(0))
+        nc.scalar.dma_start(out=xyz_sb[:], in_=xyz_view)
+
+        def load_latents(j):
+            nc.sync.dma_start(out=x_sb[:, j, :], in_=lat_view[:, j, :])
+
+        load_latents(0)
+        load_latents(1)
+        nc.sync.dma_start(
+            out=w1_codes[:].bitcast(I32),
+            in_=W1_words.rearrange("g p n t -> p g (n t)").bitcast(I32),
+        )
+        for quad in range(P // QUADRANT):
+            nc.sync.dma_start(
+                out=w1_planes[QUADRANT * quad : QUADRANT * quad + 4, :, :].bitcast(I32),
+                in_=W1_scales[:, 4 * quad : 4 * quad + 4, :].rearrange("g r n -> r g n").bitcast(I32),
+            )
+        for j in range(2, TILES):
+            load_latents(j)
+        nc.sync.dma_start(
+            out=w2_codes[:].bitcast(I32),
+            in_=W2_words[0].rearrange("p n t -> p (n t)").bitcast(I32),
+        )
+        for quad in range(P // QUADRANT):
+            nc.sync.dma_start(
+                out=w2_plane[QUADRANT * quad : QUADRANT * quad + 4, :].bitcast(I32),
+                in_=W2_scales[0, 4 * quad : 4 * quad + 4, :].bitcast(I32),
+            )
+
+        b1_bank = psum.tile([P, WIDTH], F32, tag="acc1")
+        nc.tensor.matmul(out=b1_bank[:], lhsT=ones[:], rhs=bias_rows[:, 0, :], start=True, stop=True)
+        nc.vector.tensor_copy(out=b1_spread[:], in_=b1_bank[:].rearrange("r (p t) -> r t p", t=PACK))
+        b2_bank = psum.tile([P, WIDTH], F32, tag="acc2")
+        nc.tensor.matmul(out=b2_bank[:], lhsT=ones[:], rhs=bias_rows[:, 1, :], start=True, stop=True)
+        nc.vector.tensor_copy(out=b2_spread[:], in_=b2_bank[:])
+        b2_colour = b2_spread[:].rearrange("r (q c) -> r q c", c=CHANNELS)[:, :, 11:16]
+        nc.vector.tensor_scalar_add(out=b2_colour, in0=b2_colour, scalar1=0.5)
+        nc.vector.tensor_scalar_add(out=mean_base[:], in0=xyz_sb[:], scalar1=0.5 * OFFSET_MAX)
+
+        def gaussians_of(j):
+            return o_sb[:, j, :].rearrange("r (q c) -> r q c", c=CHANNELS)
+
+        def quantise_latents(j):
+            x_words = x_sb[:, j, :].bitcast(F32)
+            xt = psum.tile([P, PASSES_1, 2, P], F32, tag="xt")
+            for g in range(PASSES_1):
+                for u in range(2):
+                    nc.tensor.transpose(
+                        xt[:, g, u, :],
+                        x_words[:, (K_PASS // 2) * g + u : (K_PASS // 2) * (g + 1) : 2],
+                        ident_f32[:],
+                    )
+            xg = stage.tile([P, PASSES_1, P, PACK], BF16, align_bytes=64)
+            xg_words = (
+                xg[:]
+                .rearrange("p g r t -> p (g r t)")
+                .bitcast(F32)
+                .rearrange("p (g r u) -> p g r u", g=PASSES_1, u=2)
+            )
+            nc.scalar.copy(out=xg_words, in_=xt[:].rearrange("p g u r -> p g r u"))
+            nc.vector.quantize_mx(
+                out=x_codes[:, j, :].bitcast(FP8X4),
+                scales=x_planes[:, j, :],
+                in_=xg[:].rearrange("p g r t -> p (g r t)"),
+            )
+
+        def first_layer(j):
+            acc1 = psum.tile([P, WIDTH], F32, tag="acc1")
+            for g in range(PASSES_1):
+                tokens = slice(P * g, P * (g + 1))
+                nc.tensor.matmul_mx(
+                    out=acc1[:],
+                    lhsT=x_codes[:, j, tokens].bitcast(FP8X4),
+                    lhsT_scale=x_planes[:, j, tokens],
+                    rhs=w1_codes[:, g, :].bitcast(FP8X4),
+                    rhs_scale=w1_planes[:, g, :],
+                    start=(g == 0),
+                    stop=(g == PASSES_1 - 1),
+                )
+            pre = stage.tile([P, PACK, P], F32)
+            nc.vector.tensor_tensor(
+                out=pre[:],
+                in0=acc1[:].rearrange("r (p t) -> r t p", t=PACK),
+                in1=b1_spread[:],
+                op=ALU.add,
+            )
+            h = stage.tile([P, PACK, P], BF16)
+            nc.scalar.activation(out=h[:], in_=pre[:], func=ACT.Silu)
+            return h
+
+        def quantise_hidden(j, h):
+            ht = psum.tile([P, PACK, P], BF16, tag="ht")
+            for t in range(PACK):
+                nc.tensor.transpose(ht[:, t, :], h[:, t, :], ident_bf16[:])
+            hg = stage.tile([P, P, PACK], BF16, align_bytes=64)
+            nc.scalar.copy(out=hg[:], in_=ht[:].rearrange("p t r -> p r t"))
+            nc.vector.quantize_mx(
+                out=h_codes[:, j, :].bitcast(FP8X4),
+                scales=h_planes[:, j, :],
+                in_=hg[:].rearrange("p r t -> p (r t)"),
+            )
+
+        def second_layer(j):
+            acc2 = psum.tile([P, WIDTH], F32, tag="acc2")
+            nc.tensor.matmul_mx(
+                out=acc2[:],
+                lhsT=h_codes[:, j, :].bitcast(FP8X4),
+                lhsT_scale=h_planes[:, j, :],
+                rhs=w2_codes[:].bitcast(FP8X4),
+                rhs_scale=w2_plane[:],
+                start=True,
+                stop=True,
+            )
+            nc.vector.tensor_tensor(out=o_sb[:, j, :], in0=acc2[:], in1=b2_spread[:], op=ALU.add)
+            rec = gaussians_of(j)
+            nc.scalar.activation(out=rec[:, :, 0:7], in_=rec[:, :, 0:7], func=ACT.Tanh, scale=0.5)
+            squares = stage.tile([P, GAUSSIANS, 4], F32)
+            nc.scalar.activation(out=squares[:], in_=rec[:, :, 7:11], func=ACT.Square)
+            nc.vector.tensor_reduce(out=norm_sq[:, j, :], in_=squares[:], axis=AXIS.X, op=ALU.add)
+
+        def finish(j):
+            rec = gaussians_of(j)
+            nc.vector.scalar_tensor_tensor(
+                out=rec[:, :, 0:3],
+                in0=rec[:, :, 0:3],
+                scalar=0.5 * OFFSET_MAX,
+                in1=mean_base[:, j, :].unsqueeze(1).to_broadcast([P, GAUSSIANS, 3]),
+                op0=ALU.mult,
+                op1=ALU.add,
+            )
+            nc.vector.tensor_scalar(
+                out=rec[:, :, 3:4], in0=rec[:, :, 3:4], scalar1=0.5, scalar2=0.5, op0=ALU.mult, op1=ALU.add
+            )
+            nc.vector.tensor_scalar(
+                out=rec[:, :, 4:7],
+                in0=rec[:, :, 4:7],
+                scalar1=0.5 * SCALE_MAX,
+                scalar2=0.5 * SCALE_MAX,
+                op0=ALU.mult,
+                op1=ALU.add,
+            )
+            nc.vector.tensor_scalar(
+                out=rec[:, :, 11:16], in0=rec[:, :, 11:16], scalar1=0.0, scalar2=1.0, op0=ALU.max, op1=ALU.min
+            )
+            nc.vector.tensor_tensor(
+                out=rec[:, :, 7:11],
+                in0=rec[:, :, 7:11],
+                in1=norm_inv[:, j, :].unsqueeze(2).to_broadcast([P, GAUSSIANS, 4]),
+                op=ALU.mult,
+            )
+            nc.sync.dma_start(out=out_view[:, j, :], in_=o_sb[:, j, :])
+
+        for j in range(TILES):
+            quantise_latents(j)
+            h = first_layer(j)
+            quantise_hidden(j, h)
+            second_layer(j)
+
+        nc.vector.tensor_scalar_max(out=norm_sq[:], in0=norm_sq[:], scalar1=NORM_FLOOR * NORM_FLOOR)
+        nc.scalar.activation(out=norm_inv[:], in_=norm_sq[:], func=ACT.Abs_reciprocal_sqrt)
+        for j in range(TILES):
+            finish(j)

@@ -11,7 +11,6 @@ U8 = mybir.dt.uint8
 FP8X4 = mybir.dt.float8_e4m3fn_x4
 ACT = mybir.ActivationFunctionType
 ALU = mybir.AluOpType
-AXIS = mybir.AxisListType
 
 P = 128
 PACK = 4
@@ -27,6 +26,10 @@ OFFSET_MAX = 0.2
 SCALE_MAX = 0.02
 NORM_FLOOR = 1e-12
 QUADRANT = 32
+LEAD = 1
+SLOT = WIDTH + 8
+STEP = 2
+AHEAD = 3
 
 FLOPS = 2 * TOKENS * (D_IN * WIDTH + WIDTH * WIDTH)
 
@@ -43,6 +46,7 @@ def tile_gaussianrenderer_kernel(
         keep = stack.enter_context(tc.tile_pool(name="keep", bufs=1))
         stage = stack.enter_context(tc.tile_pool(name="stage", bufs=3))
         psum = stack.enter_context(tc.psum_pool(name="psum", bufs=2))
+        stack.enter_context(tc.manual_schedule())
 
         x_sb = keep.tile([P, TILES, D_IN], BF16)
         x_codes = keep.tile([P, TILES, PASSES_1 * P], U32, align_bytes=64)
@@ -59,31 +63,35 @@ def tile_gaussianrenderer_kernel(
         b2_spread = keep.tile([P, WIDTH], F32)
         xyz_sb = keep.tile([P, TILES, 3], BF16)
         mean_base = keep.tile([P, TILES, 3], F32)
+        half_range = keep.tile([P, 4], F32)
         ident_f32 = keep.tile([P, P], F32)
         ident_bf16 = keep.tile([P, P], BF16)
         table_seed = keep.tile([P, 1], F32)
-        o_sb = keep.tile([P, TILES, WIDTH], F32)
+        o_sb = keep.tile([P, TILES, SLOT], F32, align_bytes=64)
         norm_sq = keep.tile([P, TILES, GAUSSIANS], F32)
         norm_inv = keep.tile([P, TILES, GAUSSIANS], F32)
 
-        nc.vector.memset(w1_planes[:].bitcast(I32), 0)
-        nc.vector.memset(w2_plane[:].bitcast(I32), 0)
         nc.vector.memset(bias_rows[:], 0.0)
-        nc.vector.memset(ones[:], 1.0)
+        nc.vector.memset(w1_planes[:].bitcast(I32), 0)
         nc.vector.memset(table_seed[:], 0.0)
+        nc.vector.memset(ones[:], 1.0)
+        nc.vector.memset(w2_plane[:].bitcast(I32), 0)
+        nc.vector.memset(half_range[:, 0:1], 0.5)
+        nc.vector.memset(half_range[:, 1:4], 0.5 * SCALE_MAX)
         make_identity(nc, ident_f32[:])
         make_identity(nc, ident_bf16[:])
+
         nc.scalar.activation(out=table_seed[:], in_=table_seed[:], func=ACT.Silu)
 
-        nc.scalar.dma_start(out=bias_rows[0:1, 0, :], in_=b1.unsqueeze(0))
-        nc.scalar.dma_start(out=bias_rows[0:1, 1, :], in_=b2.unsqueeze(0))
-        nc.scalar.dma_start(out=xyz_sb[:], in_=xyz_view)
+        def load_latents(first, count):
+            tiles = slice(first, first + count)
+            nc.sync.dma_start(out=x_sb[:, tiles, :], in_=lat_view[:, tiles, :])
 
-        def load_latents(j):
-            nc.sync.dma_start(out=x_sb[:, j, :], in_=lat_view[:, j, :])
-
-        load_latents(0)
-        load_latents(1)
+        nc.sync.dma_start(out=bias_rows[0:1, 0, :], in_=b1.unsqueeze(0))
+        nc.sync.dma_start(out=bias_rows[0:1, 1, :], in_=b2.unsqueeze(0))
+        load_latents(0, 1)
+        load_latents(1, 1)
+        load_latents(2, 1)
         nc.sync.dma_start(
             out=w1_codes[:].bitcast(I32),
             in_=W1_words.rearrange("g p n t -> p g (n t)").bitcast(I32),
@@ -93,32 +101,38 @@ def tile_gaussianrenderer_kernel(
                 out=w1_planes[QUADRANT * quad : QUADRANT * quad + 4, :, :].bitcast(I32),
                 in_=W1_scales[:, 4 * quad : 4 * quad + 4, :].rearrange("g r n -> r g n").bitcast(I32),
             )
-        for j in range(2, TILES):
-            load_latents(j)
+        load_latents(3, 1)
+        load_latents(4, 2)
+        load_latents(6, 2)
         nc.sync.dma_start(
             out=w2_codes[:].bitcast(I32),
             in_=W2_words[0].rearrange("p n t -> p (n t)").bitcast(I32),
         )
         for quad in range(P // QUADRANT):
-            nc.sync.dma_start(
-                out=w2_plane[QUADRANT * quad : QUADRANT * quad + 4, :].bitcast(I32),
-                in_=W2_scales[0, 4 * quad : 4 * quad + 4, :].bitcast(I32),
+            nc.gpsimd.dma_start(
+                out=w2_plane[QUADRANT * quad : QUADRANT * quad + 4, :].bitcast(F32),
+                in_=W2_scales[0, 4 * quad : 4 * quad + 4, :].bitcast(F32),
             )
+        nc.gpsimd.dma_start(out=xyz_sb[:], in_=xyz_view)
 
         b1_bank = psum.tile([P, WIDTH], F32, tag="acc1")
         nc.tensor.matmul(out=b1_bank[:], lhsT=ones[:], rhs=bias_rows[:, 0, :], start=True, stop=True)
-        nc.vector.tensor_copy(out=b1_spread[:], in_=b1_bank[:].rearrange("r (p t) -> r t p", t=PACK))
         b2_bank = psum.tile([P, WIDTH], F32, tag="acc2")
         nc.tensor.matmul(out=b2_bank[:], lhsT=ones[:], rhs=bias_rows[:, 1, :], start=True, stop=True)
+        nc.vector.tensor_copy(out=b1_spread[:], in_=b1_bank[:].rearrange("r (p t) -> r t p", t=PACK))
         nc.vector.tensor_copy(out=b2_spread[:], in_=b2_bank[:])
         b2_colour = b2_spread[:].rearrange("r (q c) -> r q c", c=CHANNELS)[:, :, 11:16]
         nc.vector.tensor_scalar_add(out=b2_colour, in0=b2_colour, scalar1=0.5)
-        nc.vector.tensor_scalar_add(out=mean_base[:], in0=xyz_sb[:], scalar1=0.5 * OFFSET_MAX)
+
+        live = {}
+
+        def results_of(j):
+            return o_sb[:, j, LEAD : LEAD + WIDTH]
 
         def gaussians_of(j):
-            return o_sb[:, j, :].rearrange("r (q c) -> r q c", c=CHANNELS)
+            return results_of(j).rearrange("r (q c) -> r q c", c=CHANNELS)
 
-        def quantise_latents(j):
+        def transpose_latents(j):
             x_words = x_sb[:, j, :].bitcast(F32)
             xt = psum.tile([P, PASSES_1, 2, P], F32, tag="xt")
             for g in range(PASSES_1):
@@ -128,6 +142,9 @@ def tile_gaussianrenderer_kernel(
                         x_words[:, (K_PASS // 2) * g + u : (K_PASS // 2) * (g + 1) : 2],
                         ident_f32[:],
                     )
+            live["xt", j] = xt
+
+        def group_latents(j):
             xg = stage.tile([P, PASSES_1, P, PACK], BF16, align_bytes=64)
             xg_words = (
                 xg[:]
@@ -135,11 +152,14 @@ def tile_gaussianrenderer_kernel(
                 .bitcast(F32)
                 .rearrange("p (g r u) -> p g r u", g=PASSES_1, u=2)
             )
-            nc.scalar.copy(out=xg_words, in_=xt[:].rearrange("p g u r -> p g r u"))
+            nc.scalar.copy(out=xg_words, in_=live["xt", j][:].rearrange("p g u r -> p g r u"))
+            live["xg", j] = xg
+
+        def quantise_latents(j):
             nc.vector.quantize_mx(
                 out=x_codes[:, j, :].bitcast(FP8X4),
                 scales=x_planes[:, j, :],
-                in_=xg[:].rearrange("p g r t -> p (g r t)"),
+                in_=live["xg", j][:].rearrange("p g r t -> p (g r t)"),
             )
 
         def first_layer(j):
@@ -155,27 +175,39 @@ def tile_gaussianrenderer_kernel(
                     start=(g == 0),
                     stop=(g == PASSES_1 - 1),
                 )
+            live["acc1", j] = acc1
+
+        def add_b1(j):
             pre = stage.tile([P, PACK, P], F32)
             nc.vector.tensor_tensor(
                 out=pre[:],
-                in0=acc1[:].rearrange("r (p t) -> r t p", t=PACK),
+                in0=live["acc1", j][:].rearrange("r (p t) -> r t p", t=PACK),
                 in1=b1_spread[:],
                 op=ALU.add,
             )
-            h = stage.tile([P, PACK, P], BF16)
-            nc.scalar.activation(out=h[:], in_=pre[:], func=ACT.Silu)
-            return h
+            live["pre", j] = pre
 
-        def quantise_hidden(j, h):
+        def silu(j):
+            h = stage.tile([P, PACK, P], BF16)
+            nc.scalar.activation(out=h[:], in_=live["pre", j][:], func=ACT.Silu)
+            live["h", j] = h
+
+        def transpose_hidden(j):
             ht = psum.tile([P, PACK, P], BF16, tag="ht")
             for t in range(PACK):
-                nc.tensor.transpose(ht[:, t, :], h[:, t, :], ident_bf16[:])
+                nc.tensor.transpose(ht[:, t, :], live["h", j][:, t, :], ident_bf16[:])
+            live["ht", j] = ht
+
+        def group_hidden(j):
             hg = stage.tile([P, P, PACK], BF16, align_bytes=64)
-            nc.scalar.copy(out=hg[:], in_=ht[:].rearrange("p t r -> p r t"))
+            nc.scalar.copy(out=hg[:], in_=live["ht", j][:].rearrange("p t r -> p r t"))
+            live["hg", j] = hg
+
+        def quantise_hidden(j):
             nc.vector.quantize_mx(
                 out=h_codes[:, j, :].bitcast(FP8X4),
                 scales=h_planes[:, j, :],
-                in_=hg[:].rearrange("p r t -> p (r t)"),
+                in_=live["hg", j][:].rearrange("p r t -> p (r t)"),
             )
 
         def second_layer(j):
@@ -189,14 +221,30 @@ def tile_gaussianrenderer_kernel(
                 start=True,
                 stop=True,
             )
-            nc.vector.tensor_tensor(out=o_sb[:, j, :], in0=acc2[:], in1=b2_spread[:], op=ALU.add)
+            live["acc2", j] = acc2
+
+        def add_b2(j):
+            nc.vector.tensor_tensor(
+                out=results_of(j), in0=live["acc2", j][:], in1=b2_spread[:], op=ALU.add
+            )
+
+        def tanh_of_half(j):
             rec = gaussians_of(j)
             nc.scalar.activation(out=rec[:, :, 0:7], in_=rec[:, :, 0:7], func=ACT.Tanh, scale=0.5)
-            squares = stage.tile([P, GAUSSIANS, 4], F32)
-            nc.scalar.activation(out=squares[:], in_=rec[:, :, 7:11], func=ACT.Square)
-            nc.vector.tensor_reduce(out=norm_sq[:, j, :], in_=squares[:], axis=AXIS.X, op=ALU.add)
 
-        def finish(j):
+        def square_norm(j):
+            rot = gaussians_of(j)[:, :, 7:11]
+            squares = stage.tile([P, GAUSSIANS, 4], F32)
+            nc.gpsimd.tensor_tensor(out=squares[:], in0=rot, in1=rot, op=ALU.mult)
+            pairs = stage.tile([P, GAUSSIANS, 2], F32)
+            nc.gpsimd.tensor_tensor(
+                out=pairs[:], in0=squares[:, :, 0:2], in1=squares[:, :, 2:4], op=ALU.add
+            )
+            nc.gpsimd.tensor_tensor(
+                out=norm_sq[:, j, :].unsqueeze(2), in0=pairs[:, :, 0:1], in1=pairs[:, :, 1:2], op=ALU.add
+            )
+
+        def finish_sigmoids_and_colours(j):
             rec = gaussians_of(j)
             nc.vector.scalar_tensor_tensor(
                 out=rec[:, :, 0:3],
@@ -206,35 +254,52 @@ def tile_gaussianrenderer_kernel(
                 op0=ALU.mult,
                 op1=ALU.add,
             )
-            nc.vector.tensor_scalar(
-                out=rec[:, :, 3:4], in0=rec[:, :, 3:4], scalar1=0.5, scalar2=0.5, op0=ALU.mult, op1=ALU.add
-            )
-            nc.vector.tensor_scalar(
-                out=rec[:, :, 4:7],
-                in0=rec[:, :, 4:7],
-                scalar1=0.5 * SCALE_MAX,
-                scalar2=0.5 * SCALE_MAX,
-                op0=ALU.mult,
-                op1=ALU.add,
+            nc.vector.scalar_tensor_tensor(
+                out=rec[:, :, 3:7],
+                in0=rec[:, :, 3:7],
+                scalar=1.0,
+                in1=half_range[:].unsqueeze(1).to_broadcast([P, GAUSSIANS, 4]),
+                op0=ALU.add,
+                op1=ALU.mult,
             )
             nc.vector.tensor_scalar(
                 out=rec[:, :, 11:16], in0=rec[:, :, 11:16], scalar1=0.0, scalar2=1.0, op0=ALU.max, op1=ALU.min
             )
+
+        def scale_rotation_and_store(j):
+            rot = gaussians_of(j)[:, :, 7:11]
             nc.vector.tensor_tensor(
-                out=rec[:, :, 7:11],
-                in0=rec[:, :, 7:11],
+                out=rot,
+                in0=rot,
                 in1=norm_inv[:, j, :].unsqueeze(2).to_broadcast([P, GAUSSIANS, 4]),
                 op=ALU.mult,
             )
-            nc.sync.dma_start(out=out_view[:, j, :], in_=o_sb[:, j, :])
+            nc.sync.dma_start(out=out_view[:, j, :], in_=results_of(j))
 
-        for j in range(TILES):
-            quantise_latents(j)
-            h = first_layer(j)
-            quantise_hidden(j, h)
-            second_layer(j)
+        def when_in_range(step, j):
+            if 0 <= j < TILES:
+                step(j)
 
+        for r in range(TILES + 3 * STEP + 1):
+            when_in_range(transpose_latents, r)
+            when_in_range(transpose_hidden, r - 2 * STEP)
+            when_in_range(first_layer, r - STEP)
+            when_in_range(second_layer, r - 3 * STEP)
+            when_in_range(group_latents, r - 1)
+            when_in_range(group_hidden, r - 2 * STEP - 1)
+            when_in_range(add_b1, r - STEP - 1)
+            when_in_range(add_b2, r - 3 * STEP - 1)
+            when_in_range(silu, r - STEP - 1)
+            when_in_range(tanh_of_half, r - 3 * STEP - 1)
+            when_in_range(square_norm, r - 3 * STEP - 1)
+            when_in_range(quantise_latents, r - 1)
+            when_in_range(quantise_hidden, r - 2 * STEP - 1)
+
+        nc.vector.tensor_scalar_add(out=mean_base[:], in0=xyz_sb[:], scalar1=0.5 * OFFSET_MAX)
+        for j in range(AHEAD):
+            finish_sigmoids_and_colours(j)
         nc.vector.tensor_scalar_max(out=norm_sq[:], in0=norm_sq[:], scalar1=NORM_FLOOR * NORM_FLOOR)
         nc.scalar.activation(out=norm_inv[:], in_=norm_sq[:], func=ACT.Abs_reciprocal_sqrt)
         for j in range(TILES):
-            finish(j)
+            when_in_range(finish_sigmoids_and_colours, j + AHEAD)
+            scale_rotation_and_store(j)

@@ -11,6 +11,7 @@ U8 = mybir.dt.uint8
 FP8X4 = mybir.dt.float8_e4m3fn_x4
 ACT = mybir.ActivationFunctionType
 ALU = mybir.AluOpType
+AXIS = mybir.AxisListType
 
 P = 128
 PACK = 4
@@ -29,7 +30,7 @@ QUADRANT = 32
 LEAD = 1
 SLOT = WIDTH + 8
 STEP = 2
-AHEAD = 3
+EARLY = 6
 
 FLOPS = 2 * TOKENS * (D_IN * WIDTH + WIDTH * WIDTH)
 
@@ -235,13 +236,13 @@ def tile_gaussianrenderer_kernel(
         def square_norm(j):
             rot = gaussians_of(j)[:, :, 7:11]
             squares = stage.tile([P, GAUSSIANS, 4], F32)
-            nc.gpsimd.tensor_tensor(out=squares[:], in0=rot, in1=rot, op=ALU.mult)
-            pairs = stage.tile([P, GAUSSIANS, 2], F32)
-            nc.gpsimd.tensor_tensor(
-                out=pairs[:], in0=squares[:, :, 0:2], in1=squares[:, :, 2:4], op=ALU.add
-            )
-            nc.gpsimd.tensor_tensor(
-                out=norm_sq[:, j, :].unsqueeze(2), in0=pairs[:, :, 0:1], in1=pairs[:, :, 1:2], op=ALU.add
+            nc.vector.tensor_tensor(out=squares[:], in0=rot, in1=rot, op=ALU.mult)
+            nc.vector.tensor_reduce(out=norm_sq[:, j, :], in_=squares[:], axis=AXIS.X, op=ALU.add)
+
+        def invert_norms(first, count):
+            tiles = slice(first, first + count)
+            nc.scalar.activation(
+                out=norm_inv[:, tiles, :], in_=norm_sq[:, tiles, :], func=ACT.Abs_reciprocal_sqrt
             )
 
         def finish_sigmoids_and_colours(j):
@@ -268,11 +269,13 @@ def tile_gaussianrenderer_kernel(
 
         def scale_rotation_and_store(j):
             rot = gaussians_of(j)[:, :, 7:11]
-            nc.vector.tensor_tensor(
+            nc.vector.scalar_tensor_tensor(
                 out=rot,
-                in0=rot,
-                in1=norm_inv[:, j, :].unsqueeze(2).to_broadcast([P, GAUSSIANS, 4]),
-                op=ALU.mult,
+                in0=norm_inv[:, j, :].unsqueeze(2).to_broadcast([P, GAUSSIANS, 4]),
+                scalar=1.0 / NORM_FLOOR,
+                in1=rot,
+                op0=ALU.min,
+                op1=ALU.mult,
             )
             nc.sync.dma_start(out=out_view[:, j, :], in_=results_of(j))
 
@@ -280,7 +283,7 @@ def tile_gaussianrenderer_kernel(
             if 0 <= j < TILES:
                 step(j)
 
-        for r in range(TILES + 3 * STEP + 1):
+        def pipeline_round(r):
             when_in_range(transpose_latents, r)
             when_in_range(transpose_hidden, r - 2 * STEP)
             when_in_range(first_layer, r - STEP)
@@ -289,17 +292,21 @@ def tile_gaussianrenderer_kernel(
             when_in_range(group_hidden, r - 2 * STEP - 1)
             when_in_range(add_b1, r - STEP - 1)
             when_in_range(add_b2, r - 3 * STEP - 1)
+            when_in_range(square_norm, r - 3 * STEP - 1)
             when_in_range(silu, r - STEP - 1)
             when_in_range(tanh_of_half, r - 3 * STEP - 1)
-            when_in_range(square_norm, r - 3 * STEP - 1)
             when_in_range(quantise_latents, r - 1)
             when_in_range(quantise_hidden, r - 2 * STEP - 1)
 
+        last_lag = 3 * STEP + 1
+        for r in range(EARLY + last_lag):
+            pipeline_round(r)
+        invert_norms(0, EARLY)
+        for r in range(EARLY + last_lag, TILES + last_lag):
+            pipeline_round(r)
+        invert_norms(EARLY, TILES - EARLY)
+
         nc.vector.tensor_scalar_add(out=mean_base[:], in0=xyz_sb[:], scalar1=0.5 * OFFSET_MAX)
-        for j in range(AHEAD):
-            finish_sigmoids_and_colours(j)
-        nc.vector.tensor_scalar_max(out=norm_sq[:], in0=norm_sq[:], scalar1=NORM_FLOOR * NORM_FLOOR)
-        nc.scalar.activation(out=norm_inv[:], in_=norm_sq[:], func=ACT.Abs_reciprocal_sqrt)
         for j in range(TILES):
-            when_in_range(finish_sigmoids_and_colours, j + AHEAD)
+            finish_sigmoids_and_colours(j)
             scale_rotation_and_store(j)

@@ -11,7 +11,6 @@ U8 = mybir.dt.uint8
 FP8X4 = mybir.dt.float8_e4m3fn_x4
 ACT = mybir.ActivationFunctionType
 ALU = mybir.AluOpType
-AXIS = mybir.AxisListType
 
 P = 128
 PACK = 4
@@ -88,9 +87,9 @@ def tile_gaussianrenderer_kernel(
             tiles = slice(first, first + count)
             nc.sync.dma_start(out=x_sb[:, tiles, :], in_=lat_view[:, tiles, :])
 
+        load_latents(0, 1)
         nc.sync.dma_start(out=bias_rows[0:1, 0, :], in_=b1.unsqueeze(0))
         nc.sync.dma_start(out=bias_rows[0:1, 1, :], in_=b2.unsqueeze(0))
-        load_latents(0, 1)
         load_latents(1, 1)
         load_latents(2, 1)
         nc.sync.dma_start(
@@ -116,14 +115,15 @@ def tile_gaussianrenderer_kernel(
             )
         nc.gpsimd.dma_start(out=xyz_sb[:], in_=xyz_view)
 
-        b1_bank = psum.tile([P, WIDTH], F32, tag="acc1")
-        nc.tensor.matmul(out=b1_bank[:], lhsT=ones[:], rhs=bias_rows[:, 0, :], start=True, stop=True)
-        b2_bank = psum.tile([P, WIDTH], F32, tag="acc2")
-        nc.tensor.matmul(out=b2_bank[:], lhsT=ones[:], rhs=bias_rows[:, 1, :], start=True, stop=True)
-        nc.vector.tensor_copy(out=b1_spread[:], in_=b1_bank[:].rearrange("r (p t) -> r t p", t=PACK))
-        nc.vector.tensor_copy(out=b2_spread[:], in_=b2_bank[:])
-        b2_colour = b2_spread[:].rearrange("r (q c) -> r q c", c=CHANNELS)[:, :, 11:16]
-        nc.vector.tensor_scalar_add(out=b2_colour, in0=b2_colour, scalar1=0.5)
+        def spread_biases():
+            b1_bank = psum.tile([P, WIDTH], F32, tag="acc1")
+            nc.tensor.matmul(out=b1_bank[:], lhsT=ones[:], rhs=bias_rows[:, 0, :], start=True, stop=True)
+            b2_bank = psum.tile([P, WIDTH], F32, tag="acc2")
+            nc.tensor.matmul(out=b2_bank[:], lhsT=ones[:], rhs=bias_rows[:, 1, :], start=True, stop=True)
+            nc.vector.tensor_copy(out=b1_spread[:], in_=b1_bank[:].rearrange("r (p t) -> r t p", t=PACK))
+            nc.vector.tensor_copy(out=b2_spread[:], in_=b2_bank[:])
+            b2_colour = b2_spread[:].rearrange("r (q c) -> r q c", c=CHANNELS)[:, :, 11:16]
+            nc.vector.tensor_scalar_add(out=b2_colour, in0=b2_colour, scalar1=0.5)
 
         live = {}
 
@@ -234,10 +234,15 @@ def tile_gaussianrenderer_kernel(
             nc.scalar.activation(out=rec[:, :, 0:7], in_=rec[:, :, 0:7], func=ACT.Tanh, scale=0.5)
 
         def square_norm(j):
+            engine = nc.gpsimd if j < EARLY else nc.vector
             rot = gaussians_of(j)[:, :, 7:11]
             squares = stage.tile([P, GAUSSIANS, 4], F32)
-            nc.vector.tensor_tensor(out=squares[:], in0=rot, in1=rot, op=ALU.mult)
-            nc.vector.tensor_reduce(out=norm_sq[:, j, :], in_=squares[:], axis=AXIS.X, op=ALU.add)
+            engine.tensor_tensor(out=squares[:], in0=rot, in1=rot, op=ALU.mult)
+            pairs = stage.tile([P, GAUSSIANS, 2], F32)
+            engine.tensor_tensor(out=pairs[:], in0=squares[:, :, 0:2], in1=squares[:, :, 2:4], op=ALU.add)
+            engine.tensor_tensor(
+                out=norm_sq[:, j, :].unsqueeze(2), in0=pairs[:, :, 0:1], in1=pairs[:, :, 1:2], op=ALU.add
+            )
 
         def invert_norms(first, count):
             tiles = slice(first, first + count)
@@ -294,17 +299,23 @@ def tile_gaussianrenderer_kernel(
             when_in_range(add_b2, r - 3 * STEP - 1)
             when_in_range(square_norm, r - 3 * STEP - 1)
             when_in_range(silu, r - STEP - 1)
-            when_in_range(tanh_of_half, r - 3 * STEP - 1)
+            if r - 3 * STEP - 1 < EARLY:
+                when_in_range(tanh_of_half, r - 3 * STEP - 1)
             when_in_range(quantise_latents, r - 1)
             when_in_range(quantise_hidden, r - 2 * STEP - 1)
 
         last_lag = 3 * STEP + 1
-        for r in range(EARLY + last_lag):
+        for r in range(STEP):
+            pipeline_round(r)
+        spread_biases()
+        for r in range(STEP, EARLY + last_lag):
             pipeline_round(r)
         invert_norms(0, EARLY)
         for r in range(EARLY + last_lag, TILES + last_lag):
             pipeline_round(r)
         invert_norms(EARLY, TILES - EARLY)
+        for j in range(EARLY, TILES):
+            tanh_of_half(j)
 
         nc.vector.tensor_scalar_add(out=mean_base[:], in0=xyz_sb[:], scalar1=0.5 * OFFSET_MAX)
         for j in range(TILES):

@@ -30,6 +30,7 @@ LEAD = 1
 SLOT = WIDTH + 8
 STEP = 2
 EARLY = 6
+WARM_UP = 4
 
 FLOPS = 2 * TOKENS * (D_IN * WIDTH + WIDTH * WIDTH)
 
@@ -58,7 +59,7 @@ def tile_gaussianrenderer_kernel(
         w2_codes = keep.tile([P, WIDTH], U32, align_bytes=64)
         w2_plane = keep.tile([P, WIDTH], U8, align_bytes=64)
         bias_rows = keep.tile([P, 2, WIDTH], BF16)
-        ones = keep.tile([P, P], BF16)
+        ones = keep.tile([P, WIDTH], BF16)
         b1_spread = keep.tile([P, PACK, P], F32)
         b2_spread = keep.tile([P, WIDTH], F32)
         xyz_sb = keep.tile([P, TILES, 3], BF16)
@@ -72,14 +73,18 @@ def tile_gaussianrenderer_kernel(
         norm_inv = keep.tile([P, TILES, GAUSSIANS], F32)
 
         nc.vector.memset(bias_rows[:], 0.0)
+        nc.vector.memset(ones[:], 1.0)
         nc.vector.memset(w1_planes[:].bitcast(I32), 0)
         nc.vector.memset(table_seed[:], 0.0)
-        nc.vector.memset(ones[:], 1.0)
         nc.vector.memset(w2_plane[:].bitcast(I32), 0)
         nc.vector.memset(half_range[:, 0:1], 0.5)
         nc.vector.memset(half_range[:, 1:4], 0.5 * SCALE_MAX)
         make_identity(nc, ident_f32[:])
         make_identity(nc, ident_bf16[:])
+
+        warm_bank = psum.tile([P, WIDTH], F32, tag="acc2")
+        for i in range(WARM_UP):
+            nc.tensor.matmul(out=warm_bank[:], lhsT=ones[:, 0:P], rhs=ones[:], start=True, stop=True)
 
         nc.scalar.activation(out=table_seed[:], in_=table_seed[:], func=ACT.Silu)
 
@@ -117,9 +122,9 @@ def tile_gaussianrenderer_kernel(
 
         def spread_biases():
             b1_bank = psum.tile([P, WIDTH], F32, tag="acc1")
-            nc.tensor.matmul(out=b1_bank[:], lhsT=ones[:], rhs=bias_rows[:, 0, :], start=True, stop=True)
+            nc.tensor.matmul(out=b1_bank[:], lhsT=ones[:, 0:P], rhs=bias_rows[:, 0, :], start=True, stop=True)
             b2_bank = psum.tile([P, WIDTH], F32, tag="acc2")
-            nc.tensor.matmul(out=b2_bank[:], lhsT=ones[:], rhs=bias_rows[:, 1, :], start=True, stop=True)
+            nc.tensor.matmul(out=b2_bank[:], lhsT=ones[:, 0:P], rhs=bias_rows[:, 1, :], start=True, stop=True)
             nc.vector.tensor_copy(out=b1_spread[:], in_=b1_bank[:].rearrange("r (p t) -> r t p", t=PACK))
             nc.vector.tensor_copy(out=b2_spread[:], in_=b2_bank[:])
             b2_colour = b2_spread[:].rearrange("r (q c) -> r q c", c=CHANNELS)[:, :, 11:16]

@@ -11,6 +11,7 @@ U8 = mybir.dt.uint8
 FP8X4 = mybir.dt.float8_e4m3fn_x4
 ACT = mybir.ActivationFunctionType
 ALU = mybir.AluOpType
+AXIS = mybir.AxisListType
 
 P = 128
 PACK = 4
@@ -26,11 +27,12 @@ OFFSET_MAX = 0.2
 SCALE_MAX = 0.02
 NORM_FLOOR = 1e-12
 QUADRANT = 32
+SCALE_ROWS = 4
 LEAD = 1
 SLOT = WIDTH + 8
-STEP = 2
 EARLY = 6
 WARM_UP = 4
+VECTOR_COPIES = (3,)
 
 FLOPS = 2 * TOKENS * (D_IN * WIDTH + WIDTH * WIDTH)
 
@@ -47,6 +49,7 @@ def tile_gaussianrenderer_kernel(
         keep = stack.enter_context(tc.tile_pool(name="keep", bufs=1))
         stage = stack.enter_context(tc.tile_pool(name="stage", bufs=3))
         psum = stack.enter_context(tc.psum_pool(name="psum", bufs=2))
+        psum3 = stack.enter_context(tc.psum_pool(name="psum3", bufs=3))
         stack.enter_context(tc.manual_schedule())
 
         x_sb = keep.tile([P, TILES, D_IN], BF16)
@@ -54,81 +57,81 @@ def tile_gaussianrenderer_kernel(
         x_planes = keep.tile([P, TILES, PASSES_1 * P], U8, align_bytes=64)
         h_codes = keep.tile([P, TILES, P], U32, align_bytes=64)
         h_planes = keep.tile([P, TILES, P], U8, align_bytes=64)
+        w1_raw = keep.tile([P, PASSES_1, WIDTH], U32, align_bytes=64)
         w1_codes = keep.tile([P, PASSES_1, WIDTH], U32, align_bytes=64)
-        w1_planes = keep.tile([P, PASSES_1, WIDTH], U8, align_bytes=64)
+        w1_raw_planes = keep.tile([P, WIDTH], U8, align_bytes=64)
+        w1_planes = keep.tile([P, WIDTH], U8, align_bytes=64)
         w2_codes = keep.tile([P, WIDTH], U32, align_bytes=64)
         w2_plane = keep.tile([P, WIDTH], U8, align_bytes=64)
-        bias_rows = keep.tile([P, 2, WIDTH], BF16)
+        bias_rows = keep.tile([P, WIDTH], BF16)
         ones = keep.tile([P, WIDTH], BF16)
-        b1_spread = keep.tile([P, PACK, P], F32)
+        b1_cols = keep.tile([P, PACK], BF16)
         b2_spread = keep.tile([P, WIDTH], F32)
         xyz_sb = keep.tile([P, TILES, 3], BF16)
         mean_base = keep.tile([P, TILES, 3], F32)
         half_range = keep.tile([P, 4], F32)
         ident_f32 = keep.tile([P, P], F32)
-        ident_bf16 = keep.tile([P, P], BF16)
         table_seed = keep.tile([P, 1], F32)
+        th = keep.tile([P, TILES, GAUSSIANS, 7], F32)
         o_sb = keep.tile([P, TILES, SLOT], F32, align_bytes=64)
         norm_sq = keep.tile([P, TILES, GAUSSIANS], F32)
         norm_inv = keep.tile([P, TILES, GAUSSIANS], F32)
 
-        nc.vector.memset(bias_rows[:], 0.0)
-        nc.vector.memset(ones[:], 1.0)
-        nc.vector.memset(w1_planes[:].bitcast(I32), 0)
         nc.vector.memset(table_seed[:], 0.0)
+        nc.vector.memset(w1_raw_planes[:].bitcast(I32), 0)
         nc.vector.memset(w2_plane[:].bitcast(I32), 0)
-        nc.vector.memset(half_range[:, 0:1], 0.5)
-        nc.vector.memset(half_range[:, 1:4], 0.5 * SCALE_MAX)
+        nc.vector.memset(bias_rows[:], 0.0)
+        bias_colour = bias_rows[:].rearrange("r (q c) -> r q c", c=CHANNELS)[:, :, 11:16]
+        nc.vector.memset(bias_colour[QUADRANT : QUADRANT + 1, :, :], 0.5)
+        nc.vector.memset(ones[:], 1.0)
+        nc.vector.memset(half_range[:], 0.5)
+        nc.vector.tensor_scalar(
+            out=half_range[:, 1:4], in0=half_range[:, 1:4], scalar1=SCALE_MAX, scalar2=None, op0=ALU.mult
+        )
         make_identity(nc, ident_f32[:])
-        make_identity(nc, ident_bf16[:])
 
-        warm_bank = psum.tile([P, WIDTH], F32, tag="acc2")
+        nc.scalar.dma_start(out=b1_cols[:], in_=b1.rearrange("(p t) -> p t", t=PACK))
+        nc.scalar.activation(out=table_seed[:], in_=table_seed[:], func=ACT.Silu)
+        nc.scalar.dma_start(out=bias_rows[0:1, :], in_=b2.unsqueeze(0))
+
+        warm_bank = psum3.tile([P, WIDTH], F32, tag="acc2")
         for i in range(WARM_UP):
             nc.tensor.matmul(out=warm_bank[:], lhsT=ones[:, 0:P], rhs=ones[:], start=True, stop=True)
-
-        nc.scalar.activation(out=table_seed[:], in_=table_seed[:], func=ACT.Silu)
 
         def load_latents(first, count):
             tiles = slice(first, first + count)
             nc.sync.dma_start(out=x_sb[:, tiles, :], in_=lat_view[:, tiles, :])
 
         load_latents(0, 1)
-        nc.sync.dma_start(out=bias_rows[0:1, 0, :], in_=b1.unsqueeze(0))
-        nc.sync.dma_start(out=bias_rows[0:1, 1, :], in_=b2.unsqueeze(0))
+        for quad in range(P // QUADRANT):
+            rows = slice(QUADRANT * quad, QUADRANT * quad + PASSES_1 * SCALE_ROWS)
+            nc.sync.dma_start(
+                out=w1_raw_planes[rows, :].bitcast(I32),
+                in_=W1_scales[:, SCALE_ROWS * quad : SCALE_ROWS * (quad + 1), :].bitcast(I32),
+            )
+        for g in range(PASSES_1):
+            nc.sync.dma_start(
+                out=w1_raw[:, g, :].bitcast(I32),
+                in_=W1_words[g].rearrange("p n t -> p (n t)").bitcast(I32),
+            )
         load_latents(1, 1)
         load_latents(2, 1)
-        nc.sync.dma_start(
-            out=w1_codes[:].bitcast(I32),
-            in_=W1_words.rearrange("g p n t -> p g (n t)").bitcast(I32),
-        )
-        for quad in range(P // QUADRANT):
-            nc.sync.dma_start(
-                out=w1_planes[QUADRANT * quad : QUADRANT * quad + 4, :, :].bitcast(I32),
-                in_=W1_scales[:, 4 * quad : 4 * quad + 4, :].rearrange("g r n -> r g n").bitcast(I32),
-            )
         load_latents(3, 1)
         load_latents(4, 2)
-        load_latents(6, 2)
         nc.sync.dma_start(
             out=w2_codes[:].bitcast(I32),
             in_=W2_words[0].rearrange("p n t -> p (n t)").bitcast(I32),
         )
         for quad in range(P // QUADRANT):
-            nc.gpsimd.dma_start(
-                out=w2_plane[QUADRANT * quad : QUADRANT * quad + 4, :].bitcast(F32),
-                in_=W2_scales[0, 4 * quad : 4 * quad + 4, :].bitcast(F32),
+            nc.sync.dma_start(
+                out=w2_plane[QUADRANT * quad : QUADRANT * quad + SCALE_ROWS, :].bitcast(I32),
+                in_=W2_scales[0, SCALE_ROWS * quad : SCALE_ROWS * (quad + 1), :].bitcast(I32),
             )
+        load_latents(6, 2)
         nc.gpsimd.dma_start(out=xyz_sb[:], in_=xyz_view)
-
-        def spread_biases():
-            b1_bank = psum.tile([P, WIDTH], F32, tag="acc1")
-            nc.tensor.matmul(out=b1_bank[:], lhsT=ones[:, 0:P], rhs=bias_rows[:, 0, :], start=True, stop=True)
-            b2_bank = psum.tile([P, WIDTH], F32, tag="acc2")
-            nc.tensor.matmul(out=b2_bank[:], lhsT=ones[:, 0:P], rhs=bias_rows[:, 1, :], start=True, stop=True)
-            nc.vector.tensor_copy(out=b1_spread[:], in_=b1_bank[:].rearrange("r (p t) -> r t p", t=PACK))
-            nc.vector.tensor_copy(out=b2_spread[:], in_=b2_bank[:])
-            b2_colour = b2_spread[:].rearrange("r (q c) -> r q c", c=CHANNELS)[:, :, 11:16]
-            nc.vector.tensor_scalar_add(out=b2_colour, in0=b2_colour, scalar1=0.5)
+        nc.gpsimd.tensor_scalar(
+            out=mean_base[:], in0=xyz_sb[:], scalar1=1.0, scalar2=0.5 * OFFSET_MAX, op0=ALU.mult, op1=ALU.add
+        )
 
         live = {}
 
@@ -138,9 +141,25 @@ def tile_gaussianrenderer_kernel(
         def gaussians_of(j):
             return results_of(j).rearrange("r (q c) -> r q c", c=CHANNELS)
 
+        def permute_w1():
+            nc.vector.tensor_copy(
+                out=w1_planes[:].rearrange("p (t m) -> p t m", t=PACK),
+                in_=w1_raw_planes[:].rearrange("p (m t) -> p t m", t=PACK),
+            )
+            for g in range(PASSES_1):
+                nc.vector.tensor_copy(
+                    out=w1_codes[:, g, :].rearrange("p (t m) -> p t m", t=PACK),
+                    in_=w1_raw[:, g, :].rearrange("p (m t) -> p t m", t=PACK),
+                )
+
+        def spread_b2():
+            b2_bank = psum3.tile([P, WIDTH], F32, tag="acc2")
+            nc.tensor.matmul(out=b2_bank[:], lhsT=ones[:, 0:P], rhs=bias_rows[:], start=True, stop=True)
+            nc.scalar.copy(out=b2_spread[:], in_=b2_bank[:])
+
         def transpose_latents(j):
             x_words = x_sb[:, j, :].bitcast(F32)
-            xt = psum.tile([P, PASSES_1, 2, P], F32, tag="xt")
+            xt = psum3.tile([P, PASSES_1, 2, P], F32, tag="xt")
             for g in range(PASSES_1):
                 for u in range(2):
                     nc.tensor.transpose(
@@ -158,7 +177,8 @@ def tile_gaussianrenderer_kernel(
                 .bitcast(F32)
                 .rearrange("p (g r u) -> p g r u", g=PASSES_1, u=2)
             )
-            nc.scalar.copy(out=xg_words, in_=live["xt", j][:].rearrange("p g u r -> p g r u"))
+            copy = nc.vector.tensor_copy if j in VECTOR_COPIES else nc.scalar.copy
+            copy(out=xg_words, in_=live["xt", j][:].rearrange("p g u r -> p g r u"))
             live["xg", j] = xg
 
         def quantise_latents(j):
@@ -169,44 +189,33 @@ def tile_gaussianrenderer_kernel(
             )
 
         def first_layer(j):
-            acc1 = psum.tile([P, WIDTH], F32, tag="acc1")
-            for g in range(PASSES_1):
-                tokens = slice(P * g, P * (g + 1))
-                nc.tensor.matmul_mx(
-                    out=acc1[:],
-                    lhsT=x_codes[:, j, tokens].bitcast(FP8X4),
-                    lhsT_scale=x_planes[:, j, tokens],
-                    rhs=w1_codes[:, g, :].bitcast(FP8X4),
-                    rhs_scale=w1_planes[:, g, :],
-                    start=(g == 0),
-                    stop=(g == PASSES_1 - 1),
-                )
+            acc1 = psum.tile([P, PACK, P], F32, tag="acc1")
+            for t in range(PACK):
+                cols = slice(P * t, P * (t + 1))
+                for g in range(PASSES_1):
+                    tokens = slice(P * g, P * (g + 1))
+                    nc.tensor.matmul_mx(
+                        out=acc1[:, t, :],
+                        lhsT=w1_codes[:, g, cols].bitcast(FP8X4),
+                        lhsT_scale=w1_planes[SCALE_ROWS * g :, cols],
+                        rhs=x_codes[:, j, tokens].bitcast(FP8X4),
+                        rhs_scale=x_planes[:, j, tokens],
+                        start=(g == 0),
+                        stop=(g == PASSES_1 - 1),
+                    )
             live["acc1", j] = acc1
-
-        def add_b1(j):
-            pre = stage.tile([P, PACK, P], F32)
-            nc.vector.tensor_tensor(
-                out=pre[:],
-                in0=live["acc1", j][:].rearrange("r (p t) -> r t p", t=PACK),
-                in1=b1_spread[:],
-                op=ALU.add,
-            )
-            live["pre", j] = pre
 
         def silu(j):
             h = stage.tile([P, PACK, P], BF16)
-            nc.scalar.activation(out=h[:], in_=live["pre", j][:], func=ACT.Silu)
-            live["h", j] = h
-
-        def transpose_hidden(j):
-            ht = psum.tile([P, PACK, P], BF16, tag="ht")
             for t in range(PACK):
-                nc.tensor.transpose(ht[:, t, :], live["h", j][:, t, :], ident_bf16[:])
-            live["ht", j] = ht
+                nc.scalar.activation(
+                    out=h[:, t, :], in_=live["acc1", j][:, t, :], func=ACT.Silu, bias=b1_cols[:, t : t + 1]
+                )
+            live["h", j] = h
 
         def group_hidden(j):
             hg = stage.tile([P, P, PACK], BF16, align_bytes=64)
-            nc.scalar.copy(out=hg[:], in_=live["ht", j][:].rearrange("p t r -> p r t"))
+            nc.vector.tensor_copy(out=hg[:], in_=live["h", j][:].rearrange("p t r -> p r t"))
             live["hg", j] = hg
 
         def quantise_hidden(j):
@@ -217,7 +226,7 @@ def tile_gaussianrenderer_kernel(
             )
 
         def second_layer(j):
-            acc2 = psum.tile([P, WIDTH], F32, tag="acc2")
+            acc2 = psum3.tile([P, WIDTH], F32, tag="acc2")
             nc.tensor.matmul_mx(
                 out=acc2[:],
                 lhsT=h_codes[:, j, :].bitcast(FP8X4),
@@ -235,17 +244,17 @@ def tile_gaussianrenderer_kernel(
             )
 
         def tanh_of_half(j):
-            rec = gaussians_of(j)
-            nc.scalar.activation(out=rec[:, :, 0:7], in_=rec[:, :, 0:7], func=ACT.Tanh, scale=0.5)
+            nc.scalar.activation(
+                out=th[:, j, :, :], in_=gaussians_of(j)[:, :, 0:7], func=ACT.Tanh, scale=0.5
+            )
 
         def square_norm(j):
-            engine = nc.gpsimd if j < EARLY else nc.vector
             rot = gaussians_of(j)[:, :, 7:11]
             squares = stage.tile([P, GAUSSIANS, 4], F32)
-            engine.tensor_tensor(out=squares[:], in0=rot, in1=rot, op=ALU.mult)
+            nc.gpsimd.tensor_tensor(out=squares[:], in0=rot, in1=rot, op=ALU.mult)
             pairs = stage.tile([P, GAUSSIANS, 2], F32)
-            engine.tensor_tensor(out=pairs[:], in0=squares[:, :, 0:2], in1=squares[:, :, 2:4], op=ALU.add)
-            engine.tensor_tensor(
+            nc.gpsimd.tensor_tensor(out=pairs[:], in0=squares[:, :, 0:2], in1=squares[:, :, 2:4], op=ALU.add)
+            nc.gpsimd.tensor_tensor(
                 out=norm_sq[:, j, :].unsqueeze(2), in0=pairs[:, :, 0:1], in1=pairs[:, :, 1:2], op=ALU.add
             )
 
@@ -255,11 +264,17 @@ def tile_gaussianrenderer_kernel(
                 out=norm_inv[:, tiles, :], in_=norm_sq[:, tiles, :], func=ACT.Abs_reciprocal_sqrt
             )
 
-        def finish_sigmoids_and_colours(j):
+        def clip_colours(j):
+            colour = gaussians_of(j)[:, :, 11:16]
+            nc.vector.tensor_scalar(
+                out=colour, in0=colour, scalar1=0.0, scalar2=1.0, op0=ALU.max, op1=ALU.min
+            )
+
+        def finish_sigmoids(j):
             rec = gaussians_of(j)
             nc.vector.scalar_tensor_tensor(
                 out=rec[:, :, 0:3],
-                in0=rec[:, :, 0:3],
+                in0=th[:, j, :, 0:3],
                 scalar=0.5 * OFFSET_MAX,
                 in1=mean_base[:, j, :].unsqueeze(1).to_broadcast([P, GAUSSIANS, 3]),
                 op0=ALU.mult,
@@ -267,14 +282,11 @@ def tile_gaussianrenderer_kernel(
             )
             nc.vector.scalar_tensor_tensor(
                 out=rec[:, :, 3:7],
-                in0=rec[:, :, 3:7],
+                in0=th[:, j, :, 3:7],
                 scalar=1.0,
                 in1=half_range[:].unsqueeze(1).to_broadcast([P, GAUSSIANS, 4]),
                 op0=ALU.add,
                 op1=ALU.mult,
-            )
-            nc.vector.tensor_scalar(
-                out=rec[:, :, 11:16], in0=rec[:, :, 11:16], scalar1=0.0, scalar2=1.0, op0=ALU.max, op1=ALU.min
             )
 
         def scale_rotation_and_store(j):
@@ -295,34 +307,28 @@ def tile_gaussianrenderer_kernel(
 
         def pipeline_round(r):
             when_in_range(transpose_latents, r)
-            when_in_range(transpose_hidden, r - 2 * STEP)
-            when_in_range(first_layer, r - STEP)
-            when_in_range(second_layer, r - 3 * STEP)
-            when_in_range(group_latents, r - 1)
-            when_in_range(group_hidden, r - 2 * STEP - 1)
-            when_in_range(add_b1, r - STEP - 1)
-            when_in_range(add_b2, r - 3 * STEP - 1)
-            when_in_range(square_norm, r - 3 * STEP - 1)
-            when_in_range(silu, r - STEP - 1)
-            if r - 3 * STEP - 1 < EARLY:
-                when_in_range(tanh_of_half, r - 3 * STEP - 1)
-            when_in_range(quantise_latents, r - 1)
-            when_in_range(quantise_hidden, r - 2 * STEP - 1)
+            when_in_range(add_b2, r - 5)
+            when_in_range(group_latents, r)
+            if r == 0:
+                spread_b2()
+                permute_w1()
+            when_in_range(first_layer, r - 2)
+            when_in_range(second_layer, r - 4)
+            when_in_range(group_hidden, r - 3)
+            when_in_range(clip_colours, r - 6)
+            when_in_range(tanh_of_half, r - 7)
+            when_in_range(quantise_latents, r)
+            when_in_range(quantise_hidden, r - 3)
+            when_in_range(square_norm, r - 6)
+            when_in_range(silu, r - 2)
 
-        last_lag = 3 * STEP + 1
-        for r in range(STEP):
-            pipeline_round(r)
-        spread_biases()
-        for r in range(STEP, EARLY + last_lag):
+        last_lag = 7
+        for r in range(EARLY + last_lag - 1):
             pipeline_round(r)
         invert_norms(0, EARLY)
-        for r in range(EARLY + last_lag, TILES + last_lag):
+        for r in range(EARLY + last_lag - 1, TILES + last_lag):
             pipeline_round(r)
         invert_norms(EARLY, TILES - EARLY)
-        for j in range(EARLY, TILES):
-            tanh_of_half(j)
-
-        nc.vector.tensor_scalar_add(out=mean_base[:], in0=xyz_sb[:], scalar1=0.5 * OFFSET_MAX)
         for j in range(TILES):
-            finish_sigmoids_and_colours(j)
+            finish_sigmoids(j)
             scale_rotation_and_store(j)

@@ -251,12 +251,8 @@ def tile_gaussianrenderer_kernel(
         def square_norm(j):
             rot = gaussians_of(j)[:, :, 7:11]
             squares = stage.tile([P, GAUSSIANS, 4], F32)
-            nc.gpsimd.tensor_tensor(out=squares[:], in0=rot, in1=rot, op=ALU.mult)
-            pairs = stage.tile([P, GAUSSIANS, 2], F32)
-            nc.gpsimd.tensor_tensor(out=pairs[:], in0=squares[:, :, 0:2], in1=squares[:, :, 2:4], op=ALU.add)
-            nc.gpsimd.tensor_tensor(
-                out=norm_sq[:, j, :].unsqueeze(2), in0=pairs[:, :, 0:1], in1=pairs[:, :, 1:2], op=ALU.add
-            )
+            nc.scalar.activation(out=squares[:], in_=rot, func=ACT.Square)
+            nc.vector.tensor_reduce(out=norm_sq[:, j, :], in_=squares[:], op=ALU.add, axis=AXIS.X)
 
         def invert_norms(first, count):
             tiles = slice(first, first + count)

@@ -30,9 +30,11 @@ QUADRANT = 32
 SCALE_ROWS = 4
 LEAD = 1
 SLOT = WIDTH + 8
-EARLY = 6
 WARM_UP = 4
-VECTOR_COPIES = (3,)
+KEEP_WARM = 2
+RUN = 4
+AHEAD = 2
+EARLY = 6
 
 FLOPS = 2 * TOKENS * (D_IN * WIDTH + WIDTH * WIDTH)
 
@@ -92,7 +94,6 @@ def tile_gaussianrenderer_kernel(
 
         nc.scalar.dma_start(out=b1_cols[:], in_=b1.rearrange("(p t) -> p t", t=PACK))
         nc.scalar.activation(out=table_seed[:], in_=table_seed[:], func=ACT.Silu)
-        nc.scalar.dma_start(out=bias_rows[0:1, :], in_=b2.unsqueeze(0))
 
         warm_bank = psum3.tile([P, WIDTH], F32, tag="acc2")
         for i in range(WARM_UP):
@@ -103,6 +104,7 @@ def tile_gaussianrenderer_kernel(
             nc.sync.dma_start(out=x_sb[:, tiles, :], in_=lat_view[:, tiles, :])
 
         load_latents(0, 1)
+        nc.sync.dma_start(out=bias_rows[0:1, :], in_=b2.unsqueeze(0))
         for quad in range(P // QUADRANT):
             rows = slice(QUADRANT * quad, QUADRANT * quad + PASSES_1 * SCALE_ROWS)
             nc.sync.dma_start(
@@ -148,14 +150,17 @@ def tile_gaussianrenderer_kernel(
             )
             for g in range(PASSES_1):
                 nc.vector.tensor_copy(
-                    out=w1_codes[:, g, :].rearrange("p (t m) -> p t m", t=PACK),
-                    in_=w1_raw[:, g, :].rearrange("p (m t) -> p t m", t=PACK),
+                    out=w1_codes[:, g, :].rearrange("p (t c i) -> p c t i", t=PACK, i=RUN),
+                    in_=w1_raw[:, g, :].rearrange("p (c i t) -> p c t i", t=PACK, i=RUN),
                 )
 
         def spread_b2():
             b2_bank = psum3.tile([P, WIDTH], F32, tag="acc2")
             nc.tensor.matmul(out=b2_bank[:], lhsT=ones[:, 0:P], rhs=bias_rows[:], start=True, stop=True)
-            nc.scalar.copy(out=b2_spread[:], in_=b2_bank[:])
+            live["b2"] = b2_bank
+            keep_bank = psum3.tile([P, WIDTH], F32, tag="acc2")
+            for i in range(KEEP_WARM):
+                nc.tensor.matmul(out=keep_bank[:], lhsT=ones[:, 0:P], rhs=ones[:], start=True, stop=True)
 
         def transpose_latents(j):
             x_words = x_sb[:, j, :].bitcast(F32)
@@ -177,8 +182,7 @@ def tile_gaussianrenderer_kernel(
                 .bitcast(F32)
                 .rearrange("p (g r u) -> p g r u", g=PASSES_1, u=2)
             )
-            copy = nc.vector.tensor_copy if j in VECTOR_COPIES else nc.scalar.copy
-            copy(out=xg_words, in_=live["xt", j][:].rearrange("p g u r -> p g r u"))
+            nc.scalar.copy(out=xg_words, in_=live["xt", j][:].rearrange("p g u r -> p g r u"))
             live["xg", j] = xg
 
         def quantise_latents(j):
@@ -215,7 +219,10 @@ def tile_gaussianrenderer_kernel(
 
         def group_hidden(j):
             hg = stage.tile([P, P, PACK], BF16, align_bytes=64)
-            nc.vector.tensor_copy(out=hg[:], in_=live["h", j][:].rearrange("p t r -> p r t"))
+            nc.vector.tensor_copy(
+                out=hg[:].rearrange("p (c i) t -> p c t i", i=RUN),
+                in_=live["h", j][:].rearrange("p t (c i) -> p c t i", i=RUN),
+            )
             live["hg", j] = hg
 
         def quantise_hidden(j):
@@ -248,11 +255,15 @@ def tile_gaussianrenderer_kernel(
                 out=th[:, j, :, :], in_=gaussians_of(j)[:, :, 0:7], func=ACT.Tanh, scale=0.5
             )
 
-        def square_norm(j):
-            rot = gaussians_of(j)[:, :, 7:11]
+        def square_rotation(j):
             squares = stage.tile([P, GAUSSIANS, 4], F32)
-            nc.scalar.activation(out=squares[:], in_=rot, func=ACT.Square)
-            nc.vector.tensor_reduce(out=norm_sq[:, j, :], in_=squares[:], op=ALU.add, axis=AXIS.X)
+            nc.scalar.activation(out=squares[:], in_=gaussians_of(j)[:, :, 7:11], func=ACT.Square)
+            live["squares", j] = squares
+
+        def sum_squares(j):
+            nc.vector.tensor_reduce(
+                out=norm_sq[:, j, :], in_=live["squares", j][:], op=ALU.add, axis=AXIS.X
+            )
 
         def invert_norms(first, count):
             tiles = slice(first, first + count)
@@ -303,28 +314,44 @@ def tile_gaussianrenderer_kernel(
 
         def pipeline_round(r):
             when_in_range(transpose_latents, r)
-            when_in_range(add_b2, r - 5)
-            when_in_range(group_latents, r)
             if r == 0:
                 spread_b2()
-                permute_w1()
+            when_in_range(square_rotation, r - 7)
+            when_in_range(group_latents, r - 1)
+            if r == 1:
+                nc.scalar.copy(out=b2_spread[:], in_=live["b2"][:])
+            when_in_range(tanh_of_half, r - 7)
+            when_in_range(group_hidden, r - 4)
+            when_in_range(silu, r - 3)
+            if r - 7 < EARLY:
+                when_in_range(sum_squares, r - 7)
+            when_in_range(quantise_hidden, r - 4)
+            when_in_range(add_b2, r - 5)
+            when_in_range(quantise_latents, r - 1)
             when_in_range(first_layer, r - 2)
             when_in_range(second_layer, r - 4)
-            when_in_range(group_hidden, r - 3)
-            when_in_range(clip_colours, r - 6)
-            when_in_range(tanh_of_half, r - 7)
-            when_in_range(quantise_latents, r)
-            when_in_range(quantise_hidden, r - 3)
-            when_in_range(square_norm, r - 6)
-            when_in_range(silu, r - 2)
 
-        last_lag = 7
-        for r in range(EARLY + last_lag - 1):
+        for r in range(TILES + 7):
+            if r == 1:
+                permute_w1()
             pipeline_round(r)
-        invert_norms(0, EARLY)
-        for r in range(EARLY + last_lag - 1, TILES + last_lag):
-            pipeline_round(r)
-        invert_norms(EARLY, TILES - EARLY)
-        for j in range(TILES):
+            if r == EARLY + 6:
+                invert_norms(0, EARLY)
+
+        def finish(j):
+            clip_colours(j)
             finish_sigmoids(j)
+
+        for j in range(AHEAD):
+            finish(j)
+        for j in range(EARLY):
+            if j + AHEAD < EARLY:
+                finish(j + AHEAD)
+            scale_rotation_and_store(j)
+        for j in range(EARLY, TILES):
+            sum_squares(j)
+        invert_norms(EARLY, TILES - EARLY)
+        for j in range(EARLY, TILES):
+            finish(j)
+        for j in range(EARLY, TILES):
             scale_rotation_and_store(j)

@@ -30,8 +30,7 @@ QUADRANT = 32
 SCALE_ROWS = 4
 LEAD = 1
 SLOT = WIDTH + 8
-WARM_UP = 4
-KEEP_WARM = 2
+WARM_UP = 3
 RUN = 4
 AHEAD = 2
 EARLY = 6
@@ -92,31 +91,26 @@ def tile_gaussianrenderer_kernel(
         )
         make_identity(nc, ident_f32[:])
 
-        nc.scalar.dma_start(out=b1_cols[:], in_=b1.rearrange("(p t) -> p t", t=PACK))
         nc.scalar.activation(out=table_seed[:], in_=table_seed[:], func=ACT.Silu)
-
-        warm_bank = psum3.tile([P, WIDTH], F32, tag="acc2")
-        for i in range(WARM_UP):
-            nc.tensor.matmul(out=warm_bank[:], lhsT=ones[:, 0:P], rhs=ones[:], start=True, stop=True)
 
         def load_latents(first, count):
             tiles = slice(first, first + count)
             nc.sync.dma_start(out=x_sb[:, tiles, :], in_=lat_view[:, tiles, :])
 
         load_latents(0, 1)
-        nc.sync.dma_start(out=bias_rows[0:1, :], in_=b2.unsqueeze(0))
         for quad in range(P // QUADRANT):
             rows = slice(QUADRANT * quad, QUADRANT * quad + PASSES_1 * SCALE_ROWS)
             nc.sync.dma_start(
                 out=w1_raw_planes[rows, :].bitcast(I32),
                 in_=W1_scales[:, SCALE_ROWS * quad : SCALE_ROWS * (quad + 1), :].bitcast(I32),
             )
-        for g in range(PASSES_1):
-            nc.sync.dma_start(
-                out=w1_raw[:, g, :].bitcast(I32),
-                in_=W1_words[g].rearrange("p n t -> p (n t)").bitcast(I32),
-            )
+        nc.sync.dma_start(
+            out=w1_raw[:].bitcast(I32),
+            in_=W1_words.rearrange("g p n t -> p g (n t)").bitcast(I32),
+        )
         load_latents(1, 1)
+        nc.sync.dma_start(out=bias_rows[0:1, :], in_=b2.unsqueeze(0))
+        nc.sync.dma_start(out=b1_cols[:], in_=b1.rearrange("(p t) -> p t", t=PACK))
         load_latents(2, 1)
         load_latents(3, 1)
         load_latents(4, 2)
@@ -157,10 +151,12 @@ def tile_gaussianrenderer_kernel(
         def spread_b2():
             b2_bank = psum3.tile([P, WIDTH], F32, tag="acc2")
             nc.tensor.matmul(out=b2_bank[:], lhsT=ones[:, 0:P], rhs=bias_rows[:], start=True, stop=True)
-            live["b2"] = b2_bank
-            keep_bank = psum3.tile([P, WIDTH], F32, tag="acc2")
-            for i in range(KEEP_WARM):
-                nc.tensor.matmul(out=keep_bank[:], lhsT=ones[:, 0:P], rhs=ones[:], start=True, stop=True)
+            nc.scalar.copy(out=b2_spread[:], in_=b2_bank[:])
+
+        def warm_up():
+            warm_bank = psum3.tile([P, WIDTH], F32, tag="acc2")
+            for i in range(WARM_UP):
+                nc.tensor.matmul(out=warm_bank[:], lhsT=ones[:, 0:P], rhs=ones[:], start=True, stop=True)
 
         def transpose_latents(j):
             x_words = x_sb[:, j, :].bitcast(F32)
@@ -315,11 +311,11 @@ def tile_gaussianrenderer_kernel(
         def pipeline_round(r):
             when_in_range(transpose_latents, r)
             if r == 0:
-                spread_b2()
+                warm_up()
             when_in_range(square_rotation, r - 7)
             when_in_range(group_latents, r - 1)
-            if r == 1:
-                nc.scalar.copy(out=b2_spread[:], in_=live["b2"][:])
+            if r == 2:
+                spread_b2()
             when_in_range(tanh_of_half, r - 7)
             when_in_range(group_hidden, r - 4)
             when_in_range(silu, r - 3)

@@ -30,9 +30,9 @@ QUADRANT = 32
 SCALE_ROWS = 4
 LEAD = 1
 SLOT = WIDTH + 8
-WARM_UP = 3
+WARM_UP = 1
 RUN = 4
-AHEAD = 2
+AHEAD = 3
 EARLY = 6
 
 FLOPS = 2 * TOKENS * (D_IN * WIDTH + WIDTH * WIDTH)
@@ -104,11 +104,11 @@ def tile_gaussianrenderer_kernel(
                 out=w1_raw_planes[rows, :].bitcast(I32),
                 in_=W1_scales[:, SCALE_ROWS * quad : SCALE_ROWS * (quad + 1), :].bitcast(I32),
             )
+        load_latents(1, 1)
         nc.sync.dma_start(
             out=w1_raw[:].bitcast(I32),
             in_=W1_words.rearrange("g p n t -> p g (n t)").bitcast(I32),
         )
-        load_latents(1, 1)
         nc.sync.dma_start(out=bias_rows[0:1, :], in_=b2.unsqueeze(0))
         nc.sync.dma_start(out=b1_cols[:], in_=b1.rearrange("(p t) -> p t", t=PACK))
         load_latents(2, 1)
@@ -151,7 +151,7 @@ def tile_gaussianrenderer_kernel(
         def spread_b2():
             b2_bank = psum3.tile([P, WIDTH], F32, tag="acc2")
             nc.tensor.matmul(out=b2_bank[:], lhsT=ones[:, 0:P], rhs=bias_rows[:], start=True, stop=True)
-            nc.scalar.copy(out=b2_spread[:], in_=b2_bank[:])
+            live["b2"] = b2_bank
 
         def warm_up():
             warm_bank = psum3.tile([P, WIDTH], F32, tag="acc2")
@@ -310,44 +310,47 @@ def tile_gaussianrenderer_kernel(
 
         def pipeline_round(r):
             when_in_range(transpose_latents, r)
-            if r == 0:
+            if r == 1:
                 warm_up()
-            when_in_range(square_rotation, r - 7)
-            when_in_range(group_latents, r - 1)
-            if r == 2:
                 spread_b2()
-            when_in_range(tanh_of_half, r - 7)
+            when_in_range(group_latents, r - 1)
             when_in_range(group_hidden, r - 4)
-            when_in_range(silu, r - 3)
             if r - 7 < EARLY:
                 when_in_range(sum_squares, r - 7)
             when_in_range(quantise_hidden, r - 4)
-            when_in_range(add_b2, r - 5)
+            when_in_range(silu, r - 3)
+            if r - 6 < EARLY:
+                when_in_range(square_rotation, r - 6)
             when_in_range(quantise_latents, r - 1)
+            if r == 2:
+                nc.vector.tensor_copy(out=b2_spread[:], in_=live["b2"][:])
+            when_in_range(add_b2, r - 5)
+            if r - 8 < EARLY:
+                when_in_range(tanh_of_half, r - 8)
+            if r == 1:
+                permute_w1()
             when_in_range(first_layer, r - 2)
             when_in_range(second_layer, r - 4)
 
-        for r in range(TILES + 7):
-            if r == 1:
-                permute_w1()
+        for r in range(TILES + 6):
             pipeline_round(r)
-            if r == EARLY + 6:
-                invert_norms(0, EARLY)
 
         def finish(j):
             clip_colours(j)
             finish_sigmoids(j)
 
+        invert_norms(0, EARLY)
+        for j in range(EARLY, TILES):
+            square_rotation(j)
         for j in range(AHEAD):
             finish(j)
-        for j in range(EARLY):
-            if j + AHEAD < EARLY:
-                finish(j + AHEAD)
-            scale_rotation_and_store(j)
+        scale_rotation_and_store(0)
         for j in range(EARLY, TILES):
             sum_squares(j)
         invert_norms(EARLY, TILES - EARLY)
         for j in range(EARLY, TILES):
-            finish(j)
-        for j in range(EARLY, TILES):
+            tanh_of_half(j)
+        for j in range(1, TILES):
+            if j >= AHEAD:
+                finish(j)
             scale_rotation_and_store(j)

@@ -32,7 +32,7 @@ LEAD = 1
 SLOT = WIDTH + 8
 WARM_UP = 1
 RUN = 4
-AHEAD = 3
+CLIPPED = 6
 EARLY = 6
 
 FLOPS = 2 * TOKENS * (D_IN * WIDTH + WIDTH * WIDTH)
@@ -314,9 +314,13 @@ def tile_gaussianrenderer_kernel(
                 warm_up()
                 spread_b2()
             when_in_range(group_latents, r - 1)
+            if r - 7 < EARLY:
+                when_in_range(tanh_of_half, r - 7)
             when_in_range(group_hidden, r - 4)
             if r - 7 < EARLY:
                 when_in_range(sum_squares, r - 7)
+            if r - 6 < CLIPPED:
+                when_in_range(clip_colours, r - 6)
             when_in_range(quantise_hidden, r - 4)
             when_in_range(silu, r - 3)
             if r - 6 < EARLY:
@@ -324,33 +328,30 @@ def tile_gaussianrenderer_kernel(
             when_in_range(quantise_latents, r - 1)
             if r == 2:
                 nc.vector.tensor_copy(out=b2_spread[:], in_=live["b2"][:])
+            if r - 5 == TILES - 1:
+                finish_sigmoids(0)
             when_in_range(add_b2, r - 5)
-            if r - 8 < EARLY:
-                when_in_range(tanh_of_half, r - 8)
             if r == 1:
                 permute_w1()
             when_in_range(first_layer, r - 2)
             when_in_range(second_layer, r - 4)
 
-        for r in range(TILES + 6):
+        for r in range(TILES + 5):
             pipeline_round(r)
-
-        def finish(j):
-            clip_colours(j)
-            finish_sigmoids(j)
 
         invert_norms(0, EARLY)
         for j in range(EARLY, TILES):
             square_rotation(j)
-        for j in range(AHEAD):
-            finish(j)
         scale_rotation_and_store(0)
+        finish_sigmoids(1)
+        scale_rotation_and_store(1)
         for j in range(EARLY, TILES):
             sum_squares(j)
         invert_norms(EARLY, TILES - EARLY)
         for j in range(EARLY, TILES):
             tanh_of_half(j)
-        for j in range(1, TILES):
-            if j >= AHEAD:
-                finish(j)
+        for j in range(2, TILES):
+            if j >= CLIPPED:
+                clip_colours(j)
+            finish_sigmoids(j)
             scale_rotation_and_store(j)

@@ -32,8 +32,8 @@ LEAD = 1
 SLOT = WIDTH + 8
 WARM_UP = 1
 RUN = 4
-CLIPPED = 6
-EARLY = 6
+CLIPPED = 5
+EARLY = 5
 
 FLOPS = 2 * TOKENS * (D_IN * WIDTH + WIDTH * WIDTH)
 
@@ -75,6 +75,7 @@ def tile_gaussianrenderer_kernel(
         table_seed = keep.tile([P, 1], F32)
         th = keep.tile([P, TILES, GAUSSIANS, 7], F32)
         o_sb = keep.tile([P, TILES, SLOT], F32, align_bytes=64)
+        squares = keep.tile([P, TILES, GAUSSIANS, 4], F32)
         norm_sq = keep.tile([P, TILES, GAUSSIANS], F32)
         norm_inv = keep.tile([P, TILES, GAUSSIANS], F32)
 
@@ -252,13 +253,11 @@ def tile_gaussianrenderer_kernel(
             )
 
         def square_rotation(j):
-            squares = stage.tile([P, GAUSSIANS, 4], F32)
-            nc.scalar.activation(out=squares[:], in_=gaussians_of(j)[:, :, 7:11], func=ACT.Square)
-            live["squares", j] = squares
+            nc.scalar.activation(out=squares[:, j, :, :], in_=gaussians_of(j)[:, :, 7:11], func=ACT.Square)
 
         def sum_squares(j):
             nc.vector.tensor_reduce(
-                out=norm_sq[:, j, :], in_=live["squares", j][:], op=ALU.add, axis=AXIS.X
+                out=norm_sq[:, j, :], in_=squares[:, j, :, :], op=ALU.add, axis=AXIS.X
             )
 
         def invert_norms(first, count):
@@ -314,25 +313,23 @@ def tile_gaussianrenderer_kernel(
                 warm_up()
                 spread_b2()
             when_in_range(group_latents, r - 1)
-            if r - 7 < EARLY:
-                when_in_range(tanh_of_half, r - 7)
             when_in_range(group_hidden, r - 4)
-            if r - 7 < EARLY:
-                when_in_range(sum_squares, r - 7)
+            if r - 8 < EARLY:
+                when_in_range(sum_squares, r - 8)
             if r - 6 < CLIPPED:
                 when_in_range(clip_colours, r - 6)
+            when_in_range(quantise_latents, r - 1)
+            if r == 1:
+                permute_w1()
+            if r == 2:
+                nc.vector.tensor_copy(out=b2_spread[:], in_=live["b2"][:])
             when_in_range(quantise_hidden, r - 4)
+            if r - 8 < EARLY:
+                when_in_range(tanh_of_half, r - 8)
             when_in_range(silu, r - 3)
             if r - 6 < EARLY:
                 when_in_range(square_rotation, r - 6)
-            when_in_range(quantise_latents, r - 1)
-            if r == 2:
-                nc.vector.tensor_copy(out=b2_spread[:], in_=live["b2"][:])
-            if r - 5 == TILES - 1:
-                finish_sigmoids(0)
             when_in_range(add_b2, r - 5)
-            if r == 1:
-                permute_w1()
             when_in_range(first_layer, r - 2)
             when_in_range(second_layer, r - 4)
 
@@ -342,16 +339,18 @@ def tile_gaussianrenderer_kernel(
         invert_norms(0, EARLY)
         for j in range(EARLY, TILES):
             square_rotation(j)
+        finish_sigmoids(0)
         scale_rotation_and_store(0)
-        finish_sigmoids(1)
-        scale_rotation_and_store(1)
         for j in range(EARLY, TILES):
             sum_squares(j)
         invert_norms(EARLY, TILES - EARLY)
         for j in range(EARLY, TILES):
             tanh_of_half(j)
-        for j in range(2, TILES):
-            if j >= CLIPPED:
-                clip_colours(j)
+        for j in range(1, EARLY):
+            finish_sigmoids(j)
+            scale_rotation_and_store(j)
+        for j in range(EARLY, TILES):
+            clip_colours(j)
+        for j in range(EARLY, TILES):
             finish_sigmoids(j)
             scale_rotation_and_store(j)

from contextlib import ExitStack

import concourse.mybir as mybir
from concourse.masks import make_identity

F32 = mybir.dt.float32
BF16 = mybir.dt.bfloat16
I32 = mybir.dt.int32
U32 = mybir.dt.uint32
U8 = mybir.dt.uint8
FP8X4 = mybir.dt.float8_e4m3fn_x4
ACT = mybir.ActivationFunctionType
ALU = mybir.AluOpType
AXIS = mybir.AxisListType

P = 128
PACK = 4
K_PASS = P * PACK
TOKENS = 2 * 512
TILES = TOKENS // P
D_IN = 1024
WIDTH = 512
PASSES_1 = D_IN // K_PASS
GAUSSIANS = 32
CHANNELS = 16
OFFSET_MAX = 0.2
SCALE_MAX = 0.02
NORM_FLOOR = 1e-12
QUADRANT = 32
SCALE_ROWS = 4
LEAD = 1
SLOT = WIDTH + 8
WARM_UP = 1
RUN = 4
CLIPPED = 5
EARLY = 5

FLOPS = 2 * TOKENS * (D_IN * WIDTH + WIDTH * WIDTH)


def tile_gaussianrenderer_kernel(
    tc, xyzs, latents, W1_words, W1_scales, b1, W2_words, W2_scales, b2, out
):
    nc = tc.nc
    lat_view = latents.flatten_outer_dims().rearrange("(p j) d -> p j d", j=TILES)
    xyz_view = xyzs.flatten_outer_dims().rearrange("(p j) c -> p j c", j=TILES)
    out_view = out.flatten_outer_dims().rearrange("(p j q) c -> p j (q c)", j=TILES, q=GAUSSIANS)

    with ExitStack() as stack:
        keep = stack.enter_context(tc.tile_pool(name="keep", bufs=1))
        stage = stack.enter_context(tc.tile_pool(name="stage", bufs=3))
        psum = stack.enter_context(tc.psum_pool(name="psum", bufs=2))
        psum3 = stack.enter_context(tc.psum_pool(name="psum3", bufs=3))
        stack.enter_context(tc.manual_schedule())

        x_sb = keep.tile([P, TILES, D_IN], BF16)
        x_codes = keep.tile([P, TILES, PASSES_1 * P], U32, align_bytes=64)
        x_planes = keep.tile([P, TILES, PASSES_1 * P], U8, align_bytes=64)
        h_codes = keep.tile([P, TILES, P], U32, align_bytes=64)
        h_planes = keep.tile([P, TILES, P], U8, align_bytes=64)
        w1_raw = keep.tile([P, PASSES_1, WIDTH], U32, align_bytes=64)
        w1_codes = keep.tile([P, PASSES_1, WIDTH], U32, align_bytes=64)
        w1_raw_planes = keep.tile([P, WIDTH], U8, align_bytes=64)
        w1_planes = keep.tile([P, WIDTH], U8, align_bytes=64)
        w2_codes = keep.tile([P, WIDTH], U32, align_bytes=64)
        w2_plane = keep.tile([P, WIDTH], U8, align_bytes=64)
        bias_rows = keep.tile([P, WIDTH], BF16)
        ones = keep.tile([P, WIDTH], BF16)
        b1_cols = keep.tile([P, PACK], BF16)
        b2_spread = keep.tile([P, WIDTH], F32)
        xyz_sb = keep.tile([P, TILES, 3], BF16)
        mean_base = keep.tile([P, TILES, 3], F32)
        half_range = keep.tile([P, 4], F32)
        ident_f32 = keep.tile([P, P], F32)
        table_seed = keep.tile([P, 1], F32)
        th = keep.tile([P, TILES, GAUSSIANS, 7], F32)
        o_sb = keep.tile([P, TILES, SLOT], F32, align_bytes=64)
        squares = keep.tile([P, TILES, GAUSSIANS, 4], F32)
        norm_sq = keep.tile([P, TILES, GAUSSIANS], F32)
        norm_inv = keep.tile([P, TILES, GAUSSIANS], F32)

        nc.vector.memset(table_seed[:], 0.0)
        nc.vector.memset(w1_raw_planes[:].bitcast(I32), 0)
        nc.vector.memset(w2_plane[:].bitcast(I32), 0)
        nc.vector.memset(bias_rows[:], 0.0)
        bias_colour = bias_rows[:].rearrange("r (q c) -> r q c", c=CHANNELS)[:, :, 11:16]
        nc.vector.memset(bias_colour[QUADRANT : QUADRANT + 1, :, :], 0.5)
        nc.vector.memset(ones[:], 1.0)
        nc.vector.memset(half_range[:], 0.5)
        nc.vector.tensor_scalar(
            out=half_range[:, 1:4], in0=half_range[:, 1:4], scalar1=SCALE_MAX, scalar2=None, op0=ALU.mult
        )
        make_identity(nc, ident_f32[:])

        nc.scalar.activation(out=table_seed[:], in_=table_seed[:], func=ACT.Silu)

        def load_latents(first, count):
            tiles = slice(first, first + count)
            nc.sync.dma_start(out=x_sb[:, tiles, :], in_=lat_view[:, tiles, :])

        load_latents(0, 1)
        for quad in range(P // QUADRANT):
            rows = slice(QUADRANT * quad, QUADRANT * quad + PASSES_1 * SCALE_ROWS)
            nc.sync.dma_start(
                out=w1_raw_planes[rows, :].bitcast(I32),
                in_=W1_scales[:, SCALE_ROWS * quad : SCALE_ROWS * (quad + 1), :].bitcast(I32),
            )
        load_latents(1, 1)
        nc.sync.dma_start(
            out=w1_raw[:].bitcast(I32),
            in_=W1_words.rearrange("g p n t -> p g (n t)").bitcast(I32),
        )
        nc.sync.dma_start(out=bias_rows[0:1, :], in_=b2.unsqueeze(0))
        nc.sync.dma_start(out=b1_cols[:], in_=b1.rearrange("(p t) -> p t", t=PACK))
        load_latents(2, 1)
        load_latents(3, 1)
        load_latents(4, 2)
        nc.sync.dma_start(
            out=w2_codes[:].bitcast(I32),
            in_=W2_words[0].rearrange("p n t -> p (n t)").bitcast(I32),
        )
        for quad in range(P // QUADRANT):
            nc.sync.dma_start(
                out=w2_plane[QUADRANT * quad : QUADRANT * quad + SCALE_ROWS, :].bitcast(I32),
                in_=W2_scales[0, SCALE_ROWS * quad : SCALE_ROWS * (quad + 1), :].bitcast(I32),
            )
        load_latents(6, 2)
        nc.gpsimd.dma_start(out=xyz_sb[:], in_=xyz_view)
        nc.gpsimd.tensor_scalar(
            out=mean_base[:], in0=xyz_sb[:], scalar1=1.0, scalar2=0.5 * OFFSET_MAX, op0=ALU.mult, op1=ALU.add
        )

        live = {}

        def results_of(j):
            return o_sb[:, j, LEAD : LEAD + WIDTH]

        def gaussians_of(j):
            return results_of(j).rearrange("r (q c) -> r q c", c=CHANNELS)

        def permute_w1():
            nc.vector.tensor_copy(
                out=w1_planes[:].rearrange("p (t m) -> p t m", t=PACK),
                in_=w1_raw_planes[:].rearrange("p (m t) -> p t m", t=PACK),
            )
            for g in range(PASSES_1):
                nc.vector.tensor_copy(
                    out=w1_codes[:, g, :].rearrange("p (t c i) -> p c t i", t=PACK, i=RUN),
                    in_=w1_raw[:, g, :].rearrange("p (c i t) -> p c t i", t=PACK, i=RUN),
                )

        def spread_b2():
            b2_bank = psum3.tile([P, WIDTH], F32, tag="acc2")
            nc.tensor.matmul(out=b2_bank[:], lhsT=ones[:, 0:P], rhs=bias_rows[:], start=True, stop=True)
            live["b2"] = b2_bank

        def warm_up():
            warm_bank = psum3.tile([P, WIDTH], F32, tag="acc2")
            for i in range(WARM_UP):
                nc.tensor.matmul(out=warm_bank[:], lhsT=ones[:, 0:P], rhs=ones[:], start=True, stop=True)

        def transpose_latents(j):
            x_words = x_sb[:, j, :].bitcast(F32)
            xt = psum3.tile([P, PASSES_1, 2, P], F32, tag="xt")
            for g in range(PASSES_1):
                for u in range(2):
                    nc.tensor.transpose(
                        xt[:, g, u, :],
                        x_words[:, (K_PASS // 2) * g + u : (K_PASS // 2) * (g + 1) : 2],
                        ident_f32[:],
                    )
            live["xt", j] = xt

        def group_latents(j):
            xg = stage.tile([P, PASSES_1, P, PACK], BF16, align_bytes=64)
            xg_words = (
                xg[:]
                .rearrange("p g r t -> p (g r t)")
                .bitcast(F32)
                .rearrange("p (g r u) -> p g r u", g=PASSES_1, u=2)
            )
            nc.scalar.copy(out=xg_words, in_=live["xt", j][:].rearrange("p g u r -> p g r u"))
            live["xg", j] = xg

        def quantise_latents(j):
            nc.vector.quantize_mx(
                out=x_codes[:, j, :].bitcast(FP8X4),
                scales=x_planes[:, j, :],
                in_=live["xg", j][:].rearrange("p g r t -> p (g r t)"),
            )

        def first_layer(j):
            acc1 = psum.tile([P, PACK, P], F32, tag="acc1")
            for t in range(PACK):
                cols = slice(P * t, P * (t + 1))
                for g in range(PASSES_1):
                    tokens = slice(P * g, P * (g + 1))
                    nc.tensor.matmul_mx(
                        out=acc1[:, t, :],
                        lhsT=w1_codes[:, g, cols].bitcast(FP8X4),
                        lhsT_scale=w1_planes[SCALE_ROWS * g :, cols],
                        rhs=x_codes[:, j, tokens].bitcast(FP8X4),
                        rhs_scale=x_planes[:, j, tokens],
                        start=(g == 0),
                        stop=(g == PASSES_1 - 1),
                    )
            live["acc1", j] = acc1

        def silu(j):
            h = stage.tile([P, PACK, P], BF16)
            for t in range(PACK):
                nc.scalar.activation(
                    out=h[:, t, :], in_=live["acc1", j][:, t, :], func=ACT.Silu, bias=b1_cols[:, t : t + 1]
                )
            live["h", j] = h

        def group_hidden(j):
            hg = stage.tile([P, P, PACK], BF16, align_bytes=64)
            nc.vector.tensor_copy(
                out=hg[:].rearrange("p (c i) t -> p c t i", i=RUN),
                in_=live["h", j][:].rearrange("p t (c i) -> p c t i", i=RUN),
            )
            live["hg", j] = hg

        def quantise_hidden(j):
            nc.vector.quantize_mx(
                out=h_codes[:, j, :].bitcast(FP8X4),
                scales=h_planes[:, j, :],
                in_=live["hg", j][:].rearrange("p r t -> p (r t)"),
            )

        def second_layer(j):
            acc2 = psum3.tile([P, WIDTH], F32, tag="acc2")
            nc.tensor.matmul_mx(
                out=acc2[:],
                lhsT=h_codes[:, j, :].bitcast(FP8X4),
                lhsT_scale=h_planes[:, j, :],
                rhs=w2_codes[:].bitcast(FP8X4),
                rhs_scale=w2_plane[:],
                start=True,
                stop=True,
            )
            live["acc2", j] = acc2

        def add_b2(j):
            nc.vector.tensor_tensor(
                out=results_of(j), in0=live["acc2", j][:], in1=b2_spread[:], op=ALU.add
            )

        def tanh_of_half(j):
            nc.scalar.activation(
                out=th[:, j, :, :], in_=gaussians_of(j)[:, :, 0:7], func=ACT.Tanh, scale=0.5
            )

        def square_rotation(j):
            nc.scalar.activation(out=squares[:, j, :, :], in_=gaussians_of(j)[:, :, 7:11], func=ACT.Square)

        def sum_squares(j):
            nc.vector.tensor_reduce(
                out=norm_sq[:, j, :], in_=squares[:, j, :, :], op=ALU.add, axis=AXIS.X
            )

        def invert_norms(first, count):
            tiles = slice(first, first + count)
            nc.scalar.activation(
                out=norm_inv[:, tiles, :], in_=norm_sq[:, tiles, :], func=ACT.Abs_reciprocal_sqrt
            )

        def clip_colours(j):
            colour = gaussians_of(j)[:, :, 11:16]
            nc.vector.tensor_scalar(
                out=colour, in0=colour, scalar1=0.0, scalar2=1.0, op0=ALU.max, op1=ALU.min
            )

        def finish_sigmoids(j):
            rec = gaussians_of(j)
            nc.vector.scalar_tensor_tensor(
                out=rec[:, :, 0:3],
                in0=th[:, j, :, 0:3],
                scalar=0.5 * OFFSET_MAX,
                in1=mean_base[:, j, :].unsqueeze(1).to_broadcast([P, GAUSSIANS, 3]),
                op0=ALU.mult,
                op1=ALU.add,
            )
            nc.vector.scalar_tensor_tensor(
                out=rec[:, :, 3:7],
                in0=th[:, j, :, 3:7],
                scalar=1.0,
                in1=half_range[:].unsqueeze(1).to_broadcast([P, GAUSSIANS, 4]),
                op0=ALU.add,
                op1=ALU.mult,
            )

        def scale_rotation_and_store(j):
            rot = gaussians_of(j)[:, :, 7:11]
            nc.vector.scalar_tensor_tensor(
                out=rot,
                in0=norm_inv[:, j, :].unsqueeze(2).to_broadcast([P, GAUSSIANS, 4]),
                scalar=1.0 / NORM_FLOOR,
                in1=rot,
                op0=ALU.min,
                op1=ALU.mult,
            )
            nc.sync.dma_start(out=out_view[:, j, :], in_=results_of(j))

        def when_in_range(step, j):
            if 0 <= j < TILES:
                step(j)

        def pipeline_round(r):
            when_in_range(transpose_latents, r)
            if r == 1:
                warm_up()
                spread_b2()
            when_in_range(group_latents, r - 1)
            when_in_range(group_hidden, r - 4)
            if r - 8 < EARLY:
                when_in_range(sum_squares, r - 8)
            if r - 6 < CLIPPED:
                when_in_range(clip_colours, r - 6)
            when_in_range(quantise_latents, r - 1)
            if r == 1:
                permute_w1()
            if r == 2:
                nc.vector.tensor_copy(out=b2_spread[:], in_=live["b2"][:])
            when_in_range(quantise_hidden, r - 4)
            if r - 8 < EARLY:
                when_in_range(tanh_of_half, r - 8)
            when_in_range(silu, r - 3)
            if r - 6 < EARLY:
                when_in_range(square_rotation, r - 6)
            when_in_range(add_b2, r - 5)
            when_in_range(first_layer, r - 2)
            when_in_range(second_layer, r - 4)

        for r in range(TILES + 5):
            pipeline_round(r)

        invert_norms(0, EARLY)
        for j in range(EARLY, TILES):
            square_rotation(j)
        finish_sigmoids(0)
        scale_rotation_and_store(0)
        for j in range(EARLY, TILES):
            sum_squares(j)
        invert_norms(EARLY, TILES - EARLY)
        for j in range(EARLY, TILES):
            tanh_of_half(j)
        for j in range(1, EARLY):
            finish_sigmoids(j)
            scale_rotation_and_store(j)
        for j in range(EARLY, TILES):
            clip_colours(j)
        for j in range(EARLY, TILES):
            finish_sigmoids(j)
            scale_rotation_and_store(j)
